import numpy as np
import ml_dtypes


def mxq(x, axis, fmt="e4m3"):
    dtype, down = {"e4m3": (ml_dtypes.float8_e4m3fn, 7), "e5m2": (ml_dtypes.float8_e5m2, 14)}[fmt]
    v = np.moveaxis(np.asarray(x, np.float32).astype(ml_dtypes.bfloat16).astype(np.float64), axis, -1)
    blocks = v.reshape(v.shape[:-1] + (-1, 32))
    amax = np.abs(blocks).max(-1, keepdims=True)
    byte = np.maximum(np.where(amax > 0, np.frexp(amax)[1] - 1 + 127, 0) - down, 1)
    scale = np.exp2(byte - 127.0)
    codes = (blocks / scale).astype(np.float32).astype(dtype).astype(np.float64)
    return np.moveaxis((codes * scale).reshape(v.shape), -1, axis)


WIDE = False


def mx_kscale(k):
    if not WIDE:
        return np.ones(k)
    levels = np.array([10, -10, 5, -5, 0])
    a = np.random.permutation(np.resize(levels, k // 512 * 4)).reshape(k // 512, 4)
    idx = np.arange(k)
    return np.exp2(a[idx // 512, idx % 128 // 32])


BF16 = ml_dtypes.bfloat16


def bf(x):
    return np.asarray(x, np.float32).astype(BF16)


def f64(x):
    return np.asarray(x).astype(np.float64)


E2M1 = np.array([0.0, 0.5, 1.0, 1.5, 2.0, 3.0, 4.0, 6.0, -0.0, -0.5, -1.0, -1.5, -2.0, -3.0, -4.0, -6.0])


def pack_weight(w, fmt):
    k, n = w.shape
    w = f64(bf(w)).reshape(k // 32, 32, n)
    amax = np.abs(w).max(1)
    if fmt == "e4m3":
        byte = np.frexp(amax)[1] - 1 + 127 - 7
    else:
        mant, ex = np.frexp(amax / 6.0)
        byte = np.where(mant > 0.5, ex, ex - 1) + 127
    byte = np.clip(np.where(amax > 0, byte, 1), 1, 254)
    scaled = (w * np.exp2(127.0 - byte)[:, None, :]).reshape(k, n).astype(np.float32)
    by_word = np.ascontiguousarray(scaled.reshape(k // 512, 128, 4, n).transpose(0, 1, 3, 2))
    if fmt == "e4m3":
        words = by_word.astype(ml_dtypes.float8_e4m3fn).view(np.uint8)
    else:
        c = by_word.astype(ml_dtypes.float4_e2m1fn).view(np.uint8) & 0xF
        words = c[..., 0::2] | (c[..., 1::2] << 4)
    return np.ascontiguousarray(words), np.ascontiguousarray(byte.astype(np.uint8).reshape(k // 512, 16, n))


def unpack_weight(words, scales, fmt):
    g, p, n, _ = words.shape
    if fmt == "e4m3":
        vals = np.ascontiguousarray(words).view(ml_dtypes.float8_e4m3fn).astype(np.float64)
    else:
        nib = np.empty((g, p, n, 4), np.uint8)
        nib[..., 0::2] = words & 0xF
        nib[..., 1::2] = words >> 4
        vals = E2M1[nib]
    vals = vals * np.repeat(np.exp2(scales.astype(np.float64) - 127.0), 8, axis=1)[..., None]
    return vals.transpose(0, 1, 3, 2).reshape(g * 512, n)


B, S, FIN, D, AF, F, H = 2, 256, 128, 1024, 2048, 4096, 16
EPS = 1e-3
FMT = "e4m3"


def layer_norm(v, gamma, beta):
    mu = v.mean(-1, keepdims=True)
    var = v.var(-1, keepdims=True)
    return (v - mu) / np.sqrt(var + EPS) * gamma + beta


def setup_inputs():
    r = np.random.standard_normal
    t = mx_kscale(F)
    h_attn = bf(r((B, S, D)))
    W1_words, W1_scales = pack_weight(r((D, F)) / np.sqrt(D) * t, FMT)
    b1 = bf(0.1 * r(F) * t)
    W2_words, W2_scales = pack_weight(r((F, D)) / np.sqrt(F) / t[:, None], FMT)
    b2 = bf(0.1 * r(D))
    g2 = bf(1.0 + 0.1 * r(D))
    beta2 = bf(0.1 * r(D))
    return {"h_attn": h_attn,
            "W1_words": W1_words, "W1_scales": W1_scales, "b1": b1,
            "W2_words": W2_words, "W2_scales": W2_scales, "b2": b2,
            "g2": g2, "beta2": beta2}


def reference(h_attn, W1_words, W1_scales, b1, W2_words, W2_scales, b2, g2, beta2):
    h = f64(h_attn)
    hid = np.maximum((mxq(h, 2, "e4m3") @ unpack_weight(W1_words, W1_scales, FMT)) + f64(b1), 0.0)
    ffn = (mxq(hid, 2, "e4m3") @ unpack_weight(W2_words, W2_scales, FMT)) + f64(b2)
    return layer_norm(h + ffn, f64(g2), f64(beta2))

@@ -1,0 +1,340 @@
+from contextlib import ExitStack
+
+import concourse.mybir as mybir
+from concourse.masks import make_identity
+
+F32 = mybir.dt.float32
+BF16 = mybir.dt.bfloat16
+I32 = mybir.dt.int32
+U32 = mybir.dt.uint32
+U8 = mybir.dt.uint8
+FP8X4 = mybir.dt.float8_e4m3fn_x4
+ADD = mybir.AluOpType.add
+MULT = mybir.AluOpType.mult
+ACT = mybir.ActivationFunctionType
+
+P = 128
+K_PASS = 512
+N_TILE = 512
+TOKENS = 512
+D = 1024
+F = 4096
+EPS = 1e-3
+TOK_TILES = TOKENS // P
+D_PASSES = D // K_PASS
+F_CHUNKS = F // K_PASS
+D_HALVES = D // N_TILE
+PLANES_PER_TILE = 4
+
+FLOPS = 2 * TOKENS * D * F * 2
+
+
+def tile_ffnn_encoder_pc_kernel(
+    tc, h_attn, W1_words, W1_scales, b1, W2_words, W2_scales, b2, g2, beta2, out
+):
+    nc = tc.nc
+    h_rows = h_attn.flatten_outer_dims()
+    out_rows = out.flatten_outer_dims()
+
+    with ExitStack() as ctx:
+        ctx.enter_context(tc.manual_schedule())
+        keep = ctx.enter_context(tc.tile_pool(name="keep", bufs=1))
+        stream = ctx.enter_context(tc.tile_pool(name="stream", bufs=3))
+        norm = ctx.enter_context(tc.tile_pool(name="norm", bufs=2))
+        psum = ctx.enter_context(tc.psum_pool(name="psum", bufs=8))
+
+        x_sb = [keep.tile([P, D], BF16, name="x_sb%d" % m) for m in range(TOK_TILES)]
+        x_sorted = [keep.tile([P, D], BF16, name="x_sorted%d" % m) for m in range(TOK_TILES)]
+        w1_words = [
+            keep.tile([P, D_PASSES, N_TILE], U32, name="w1_words%d" % g, align_bytes=64)
+            for g in range(F_CHUNKS)
+        ]
+        w2_words = [
+            keep.tile([P, D], U32, name="w2_words%d" % g, align_bytes=64) for g in range(F_CHUNKS)
+        ]
+        w1_planes = keep.tile([P, F], U8, name="w1_planes", align_bytes=64)
+        w2_planes = [
+            keep.tile([P, D], U8, name="w2_planes%d" % j, align_bytes=64)
+            for j in range(F_CHUNKS // PLANES_PER_TILE)
+        ]
+        hq_words = [
+            keep.tile([P, D_PASSES * P], U32, name="hq_words%d" % m, align_bytes=64)
+            for m in range(TOK_TILES)
+        ]
+        hq_scales = [
+            keep.tile([P, D_PASSES * P], U8, name="hq_scales%d" % m, align_bytes=64)
+            for m in range(TOK_TILES)
+        ]
+        hidq_words = [
+            keep.tile([P, TOKENS], U32, name="hidq_words%d" % g, align_bytes=64)
+            for g in range(F_CHUNKS)
+        ]
+        hidq_scales = [
+            keep.tile([P, TOKENS], U8, name="hidq_scales%d" % g, align_bytes=64)
+            for g in range(F_CHUNKS)
+        ]
+        b1_sorted = [keep.tile([P, K_PASS], BF16, name="b1_sorted%d" % g) for g in range(F_CHUNKS)]
+        b1_rows = keep.tile([P, K_PASS], BF16, name="b1_rows")
+        b2_bc = keep.tile([P, D], BF16, name="b2_bc")
+        g2_bc = keep.tile([P, D], BF16, name="g2_bc")
+        beta2_bc = keep.tile([P, D], BF16, name="beta2_bc")
+        ident_f32 = keep.tile([P, P], F32, name="ident_f32")
+        ident_bf16 = keep.tile([P, P], BF16, name="ident_bf16")
+        eps = keep.tile([P, 1], F32, name="eps")
+        first_sqrt = keep.tile([P, 1], F32, name="first_sqrt")
+
+        nc.vector.memset(b1_rows[:], 0.0)
+        nc.vector.memset(w1_planes[:].bitcast(I32), 0)
+        nc.vector.memset(eps[:], EPS)
+        for plane_tile in w2_planes:
+            nc.vector.memset(plane_tile[:].bitcast(I32), 0)
+        make_identity(nc, ident_bf16[:])
+        make_identity(nc, ident_f32[:])
+        nc.scalar.activation(out=first_sqrt[:], in_=eps[:], func=ACT.Sqrt)
+
+        def load_h(m):
+            nc.sync.dma_start(out=x_sb[m][:], in_=h_rows[m * P : (m + 1) * P, :])
+
+        def load_w1_chunk(g):
+            by_partition = W1_words.rearrange("c p n t -> p c (n t)")
+            nc.sync.dma_start(
+                out=w1_words[g][:].bitcast(I32),
+                in_=by_partition[:, :, 4 * N_TILE * g : 4 * N_TILE * (g + 1)].bitcast(I32),
+            )
+
+        def load_planes(plane_tile, scales):
+            n_planes = scales.shape[0]
+            for quadrant in range(4):
+                nc.sync.dma_start(
+                    out=plane_tile[32 * quadrant : 32 * quadrant + 4 * n_planes, :].bitcast(I32),
+                    in_=scales[:, 4 * quadrant : 4 * quadrant + 4, :].bitcast(I32),
+                )
+
+        nc.sync.dma_start(out=b1_rows[0:F_CHUNKS, :], in_=b1.rearrange("(r c) -> r c", c=K_PASS))
+        for m in range(TOK_TILES):
+            load_h(m)
+        load_planes(w1_planes, W1_scales)
+        for g in range(F_CHUNKS):
+            load_w1_chunk(g)
+        for j in range(F_CHUNKS // PLANES_PER_TILE):
+            load_planes(w2_planes[j], W2_scales[PLANES_PER_TILE * j : PLANES_PER_TILE * (j + 1)])
+        for g in range(F_CHUNKS):
+            nc.sync.dma_start(
+                out=w2_words[g][:].bitcast(I32),
+                in_=W2_words[g].rearrange("p n t -> p (n t)").bitcast(I32),
+            )
+        nc.sync.dma_start(out=b2_bc[:], in_=b2.partition_broadcast(P))
+        nc.sync.dma_start(out=g2_bc[:], in_=g2.partition_broadcast(P))
+        nc.sync.dma_start(out=beta2_bc[:], in_=beta2.partition_broadcast(P))
+
+        def sorted_view(ap):
+            return ap.rearrange("p (u q e) -> p u q e", u=2, e=2)
+
+        def natural_as_sorted(ap):
+            return ap.rearrange("p (q u e) -> p u q e", u=2, e=2)
+
+        def broadcast_b1(g):
+            bank = psum.tile([P, N_TILE], F32, tag="bank", name="b1_bank")
+            nc.tensor.matmul(
+                out=bank[:],
+                lhsT=ident_bf16[:, g : g + 1].to_broadcast([P, P]),
+                rhs=b1_rows[:],
+                start=True,
+                stop=True,
+            )
+            nc.scalar.copy(out=sorted_view(b1_sorted[g][:]), in_=natural_as_sorted(bank[:]))
+
+        def sort_h(m):
+            nc.vector.tensor_copy(
+                out=x_sorted[m][:].bitcast(F32).rearrange("p (c u q) -> p c u q", c=D_PASSES, u=2),
+                in_=x_sb[m][:].bitcast(F32).rearrange("p (c q u) -> p c u q", c=D_PASSES, u=2),
+            )
+
+        h_grouped_tiles = {}
+
+        def transpose_h(m):
+            x_as_words = x_sorted[m][:].bitcast(F32)
+            bank = psum.tile([P, D_PASSES, 2, P], F32, tag="bank", name="hT_bank")
+            for c in range(D_PASSES):
+                for u in range(2):
+                    plane = 2 * c + u
+                    nc.tensor.transpose(
+                        bank[:, c, u, :], x_as_words[:, plane * P : (plane + 1) * P], ident_f32[:]
+                    )
+            grouped = stream.tile([P, 4 * D_PASSES * P], BF16, name="h_grouped", align_bytes=64)
+            h_grouped_tiles[m] = grouped
+            nc.vector.tensor_copy(
+                out=grouped[:].bitcast(F32).rearrange("p (c w u) -> p c w u", c=D_PASSES, u=2),
+                in_=bank[:].rearrange("p c u w -> p c w u"),
+            )
+
+        def quantise_h(m):
+            nc.vector.quantize_mx(
+                out=hq_words[m][:].bitcast(FP8X4),
+                scales=hq_scales[m][:],
+                in_=h_grouped_tiles[m][:],
+            )
+
+        hid_tiles = {}
+        grouped_tiles = {}
+
+        def first_matmul(g):
+            hid = stream.tile([P, TOK_TILES, K_PASS], BF16, name="hid")
+            hid_tiles[g] = hid
+            for m in range(TOK_TILES):
+                acc = psum.tile([P, N_TILE], F32, tag="bank", name="hid_acc")
+                for c in range(D_PASSES):
+                    nc.tensor.matmul_mx(
+                        out=acc[:],
+                        lhsT=hq_words[m][:, c * P : (c + 1) * P].bitcast(FP8X4),
+                        lhsT_scale=hq_scales[m][:, c * P : (c + 1) * P],
+                        rhs=w1_words[g][:, c, :].bitcast(FP8X4),
+                        rhs_scale=w1_planes[4 * c : P, g * N_TILE : (g + 1) * N_TILE],
+                        start=(c == 0),
+                        stop=(c == D_PASSES - 1),
+                    )
+                nc.vector.tensor_tensor(
+                    out=sorted_view(hid[:, m, :]),
+                    in0=natural_as_sorted(acc[:]),
+                    in1=sorted_view(b1_sorted[g][:]),
+                    op=ADD,
+                )
+
+        def transpose_hid(g):
+            hid = hid_tiles[g]
+            grouped = stream.tile([P, 4 * TOKENS], BF16, name="hid_grouped", align_bytes=64)
+            grouped_tiles[g] = grouped
+            for pair in range(TOK_TILES // 2):
+                bank = psum.tile([P, 2, 2 * P], F32, tag="bank", name="hidT_bank")
+                for i in range(2):
+                    hid_as_words = hid[:, 2 * pair + i, :].bitcast(F32)
+                    for u in range(2):
+                        nc.tensor.transpose(
+                            bank[:, u, i * P : (i + 1) * P],
+                            hid_as_words[:, u * P : (u + 1) * P],
+                            ident_f32[:],
+                        )
+                nc.scalar.activation(
+                    out=grouped[:, 8 * P * pair : 8 * P * (pair + 1)].rearrange(
+                        "p (w u e) -> p w u e", u=2, e=2
+                    ),
+                    in_=bank[:].bitcast(BF16).rearrange("p u (w e) -> p w u e", e=2),
+                    func=ACT.Relu,
+                )
+
+        def quantise_hid(g):
+            nc.vector.quantize_mx(
+                out=hidq_words[g][:].bitcast(FP8X4),
+                scales=hidq_scales[g][:],
+                in_=grouped_tiles[g][:],
+            )
+
+        residual_tiles = {}
+
+        def residual(m):
+            res = norm.tile([P, D], F32, name="res")
+            residual_tiles[m] = res
+            for half in range(D_HALVES):
+                cols = slice(half * N_TILE, (half + 1) * N_TILE)
+                nc.gpsimd.tensor_tensor(
+                    out=res[:, cols], in0=x_sb[m][:, cols], in1=b2_bc[:, cols], op=ADD
+                )
+
+        def second_matmul(m):
+            accs = [
+                psum.tile([P, N_TILE], F32, tag="bank", name="out_acc%d" % half)
+                for half in range(D_HALVES)
+            ]
+            for g in range(F_CHUNKS):
+                for half in range(D_HALVES):
+                    offset = 4 * (g % PLANES_PER_TILE)
+                    nc.tensor.matmul_mx(
+                        out=accs[half][:],
+                        lhsT=hidq_words[g][:, m * P : (m + 1) * P].bitcast(FP8X4),
+                        lhsT_scale=hidq_scales[g][:, m * P : (m + 1) * P],
+                        rhs=w2_words[g][:, half * N_TILE : (half + 1) * N_TILE].bitcast(FP8X4),
+                        rhs_scale=w2_planes[g // PLANES_PER_TILE][
+                            offset:P, half * N_TILE : (half + 1) * N_TILE
+                        ],
+                        start=(g == 0),
+                        stop=(g == F_CHUNKS - 1),
+                    )
+            return accs
+
+        def layer_norm(m, accs):
+            r = norm.tile([P, D], F32, name="r")
+            r_sums = norm.tile([P, D_HALVES], F32, name="r_sums")
+            for half in range(D_HALVES):
+                cols = slice(half * N_TILE, (half + 1) * N_TILE)
+                nc.vector.scalar_tensor_tensor(
+                    out=r[:, cols],
+                    in0=accs[half][:],
+                    scalar=1.0,
+                    in1=residual_tiles[m][:, cols],
+                    op0=MULT,
+                    op1=ADD,
+                    accum_out=r_sums[:, half : half + 1],
+                )
+            neg_mean = norm.tile([P, 1], F32, name="neg_mean")
+            nc.vector.tensor_scalar(
+                out=neg_mean[:],
+                in0=r_sums[:, 0:1],
+                scalar1=r_sums[:, 1:2],
+                scalar2=-1.0 / D,
+                op0=ADD,
+                op1=MULT,
+            )
+            squares = norm.tile([P, D], BF16, name="squares")
+            sum_sq = norm.tile([P, 1], F32, name="sum_sq")
+            nc.scalar.activation(
+                out=squares[:], in_=r[:], func=ACT.Square, bias=neg_mean[:, 0:1], accum_out=sum_sq[:]
+            )
+            std = norm.tile([P, 1], F32, name="std")
+            nc.scalar.activation(
+                out=std[:], in_=sum_sq[:], func=ACT.Sqrt, bias=eps[:, 0:1], scale=1.0 / D
+            )
+            scaled = norm.tile([P, D], F32, name="scaled")
+            nc.vector.scalar_tensor_tensor(
+                out=scaled[:], in0=r[:], scalar=neg_mean[:, 0:1], in1=g2_bc[:], op0=ADD, op1=MULT
+            )
+            rstd = norm.tile([P, 1], F32, name="rstd")
+            nc.vector.reciprocal(rstd[:], std[:])
+            result = norm.tile([P, D], F32, name="result")
+            for half in range(D_HALVES):
+                cols = slice(half * N_TILE, (half + 1) * N_TILE)
+                nc.vector.scalar_tensor_tensor(
+                    out=result[:, cols],
+                    in0=scaled[:, cols],
+                    scalar=rstd[:, 0:1],
+                    in1=beta2_bc[:, cols],
+                    op0=MULT,
+                    op1=ADD,
+                )
+                nc.sync.dma_start(out=out_rows[m * P : (m + 1) * P, cols], in_=result[:, cols])
+
+        for g in range(F_CHUNKS):
+            broadcast_b1(g)
+        for m in range(TOK_TILES):
+            sort_h(m)
+        for step in range(TOK_TILES + 1):
+            if step < TOK_TILES:
+                transpose_h(step)
+            if 0 <= step - 1:
+                quantise_h(step - 1)
+
+        for step in range(F_CHUNKS + 2):
+            if step < F_CHUNKS:
+                first_matmul(step)
+            if 0 <= step - 1 < F_CHUNKS:
+                transpose_hid(step - 1)
+            if 0 <= step - 2:
+                quantise_hid(step - 2)
+
+        RES_AHEAD = 2
+        for m in range(RES_AHEAD):
+            residual(m)
+        for m in range(TOK_TILES):
+            accs = second_matmul(m)
+            layer_norm(m, accs)
+            if m + RES_AHEAD < TOK_TILES:
+                residual(m + RES_AHEAD)

@@ -74,7 +74,8 @@ def tile_ffnn_encoder_pc_kernel(
             for g in range(F_CHUNKS)
         ]
         b1_sorted = [keep.tile([P, K_PASS], BF16, name="b1_sorted%d" % g) for g in range(F_CHUNKS)]
-        b1_rows = keep.tile([P, K_PASS], BF16, name="b1_rows")
+        bias_rows = keep.tile([P, N_TILE], BF16, name="bias_rows")
+        res = [keep.tile([P, D], F32, name="res%d" % m) for m in range(TOK_TILES)]
         b2_bc = keep.tile([P, D], BF16, name="b2_bc")
         g2_bc = keep.tile([P, D], BF16, name="g2_bc")
         beta2_bc = keep.tile([P, D], BF16, name="beta2_bc")
@@ -83,7 +84,7 @@ def tile_ffnn_encoder_pc_kernel(
         eps = keep.tile([P, 1], F32, name="eps")
         first_sqrt = keep.tile([P, 1], F32, name="first_sqrt")
 
-        nc.vector.memset(b1_rows[:], 0.0)
+        nc.vector.memset(bias_rows[:], 0.0)
         nc.vector.memset(w1_planes[:].bitcast(I32), 0)
         nc.vector.memset(eps[:], EPS)
         for plane_tile in w2_planes:
@@ -110,7 +111,11 @@ def tile_ffnn_encoder_pc_kernel(
                     in_=scales[:, 4 * quadrant : 4 * quadrant + 4, :].bitcast(I32),
                 )
 
-        nc.sync.dma_start(out=b1_rows[0:F_CHUNKS, :], in_=b1.rearrange("(r c) -> r c", c=K_PASS))
+        nc.sync.dma_start(out=bias_rows[0:F_CHUNKS, :], in_=b1.rearrange("(r c) -> r c", c=N_TILE))
+        nc.sync.dma_start(
+            out=bias_rows[F_CHUNKS : F_CHUNKS + D_HALVES, :],
+            in_=b2.rearrange("(r c) -> r c", c=N_TILE),
+        )
         for m in range(TOK_TILES):
             load_h(m)
         load_planes(w1_planes, W1_scales)
@@ -123,7 +128,6 @@ def tile_ffnn_encoder_pc_kernel(
                 out=w2_words[g][:].bitcast(I32),
                 in_=W2_words[g].rearrange("p n t -> p (n t)").bitcast(I32),
             )
-        nc.sync.dma_start(out=b2_bc[:], in_=b2.partition_broadcast(P))
         nc.sync.dma_start(out=g2_bc[:], in_=g2.partition_broadcast(P))
         nc.sync.dma_start(out=beta2_bc[:], in_=beta2.partition_broadcast(P))
 
@@ -133,16 +137,24 @@ def tile_ffnn_encoder_pc_kernel(
         def natural_as_sorted(ap):
             return ap.rearrange("p (q u e) -> p u q e", u=2, e=2)
 
-        def broadcast_b1(g):
-            bank = psum.tile([P, N_TILE], F32, tag="bank", name="b1_bank")
+        def broadcast_row(row):
+            bank = psum.tile([P, N_TILE], F32, tag="bank", name="bias_bank")
             nc.tensor.matmul(
                 out=bank[:],
-                lhsT=ident_bf16[:, g : g + 1].to_broadcast([P, P]),
-                rhs=b1_rows[:],
+                lhsT=ident_bf16[:, row : row + 1].to_broadcast([P, P]),
+                rhs=bias_rows[:],
                 start=True,
                 stop=True,
             )
+            return bank
+
+        def broadcast_b1(g):
+            bank = broadcast_row(g)
             nc.scalar.copy(out=sorted_view(b1_sorted[g][:]), in_=natural_as_sorted(bank[:]))
+
+        def broadcast_b2(half):
+            bank = broadcast_row(F_CHUNKS + half)
+            nc.scalar.copy(out=b2_bc[:, half * N_TILE : (half + 1) * N_TILE], in_=bank[:])
 
         def sort_h(m):
             nc.vector.tensor_copy(
@@ -193,12 +205,19 @@ def tile_ffnn_encoder_pc_kernel(
                         start=(c == 0),
                         stop=(c == D_PASSES - 1),
                     )
-                nc.vector.tensor_tensor(
-                    out=sorted_view(hid[:, m, :]),
-                    in0=natural_as_sorted(acc[:]),
-                    in1=sorted_view(b1_sorted[g][:]),
-                    op=ADD,
-                )
+                if m < TOK_TILES - 1:
+                    nc.vector.tensor_tensor(
+                        out=sorted_view(hid[:, m, :]),
+                        in0=natural_as_sorted(acc[:]),
+                        in1=sorted_view(b1_sorted[g][:]),
+                        op=ADD,
+                    )
+                else:
+                    raw = stream.tile([P, K_PASS], F32, name="hid_raw")
+                    nc.scalar.copy(out=sorted_view(raw[:]), in_=natural_as_sorted(acc[:]))
+                    nc.gpsimd.tensor_tensor(
+                        out=hid[:, m, :], in0=raw[:], in1=b1_sorted[g][:], op=ADD
+                    )
 
         def transpose_hid(g):
             hid = hid_tiles[g]
@@ -229,16 +248,11 @@ def tile_ffnn_encoder_pc_kernel(
                 in_=grouped_tiles[g][:],
             )
 
-        residual_tiles = {}
-
-        def residual(m):
-            res = norm.tile([P, D], F32, name="res")
-            residual_tiles[m] = res
-            for half in range(D_HALVES):
-                cols = slice(half * N_TILE, (half + 1) * N_TILE)
-                nc.gpsimd.tensor_tensor(
-                    out=res[:, cols], in0=x_sb[m][:, cols], in1=b2_bc[:, cols], op=ADD
-                )
+        def residual(m, half):
+            cols = slice(half * N_TILE, (half + 1) * N_TILE)
+            nc.gpsimd.tensor_tensor(
+                out=res[m][:, cols], in0=x_sb[m][:, cols], in1=b2_bc[:, cols], op=ADD
+            )
 
         def second_matmul(m):
             accs = [
@@ -270,7 +284,7 @@ def tile_ffnn_encoder_pc_kernel(
                     out=r[:, cols],
                     in0=accs[half][:],
                     scalar=1.0,
-                    in1=residual_tiles[m][:, cols],
+                    in1=res[m][:, cols],
                     op0=MULT,
                     op1=ADD,
                     accum_out=r_sums[:, half : half + 1],
@@ -314,6 +328,8 @@ def tile_ffnn_encoder_pc_kernel(
 
         for g in range(F_CHUNKS):
             broadcast_b1(g)
+        for half in range(D_HALVES):
+            broadcast_b2(half)
         for m in range(TOK_TILES):
             sort_h(m)
         for step in range(TOK_TILES + 1):
@@ -325,16 +341,12 @@ def tile_ffnn_encoder_pc_kernel(
         for step in range(F_CHUNKS + 2):
             if step < F_CHUNKS:
                 first_matmul(step)
+                residual(step // D_HALVES, step % D_HALVES)
             if 0 <= step - 1 < F_CHUNKS:
                 transpose_hid(step - 1)
             if 0 <= step - 2:
                 quantise_hid(step - 2)
 
-        RES_AHEAD = 2
-        for m in range(RES_AHEAD):
-            residual(m)
         for m in range(TOK_TILES):
             accs = second_matmul(m)
             layer_norm(m, accs)
-            if m + RES_AHEAD < TOK_TILES:
-                residual(m + RES_AHEAD)

@@ -44,7 +44,6 @@ def tile_ffnn_encoder_pc_kernel(
         psum = ctx.enter_context(tc.psum_pool(name="psum", bufs=8))
 
         x_sb = [keep.tile([P, D], BF16, name="x_sb%d" % m) for m in range(TOK_TILES)]
-        x_sorted = [keep.tile([P, D], BF16, name="x_sorted%d" % m) for m in range(TOK_TILES)]
         w1_words = [
             keep.tile([P, D_PASSES, N_TILE], U32, name="w1_words%d" % g, align_bytes=64)
             for g in range(F_CHUNKS)
@@ -52,7 +51,9 @@ def tile_ffnn_encoder_pc_kernel(
         w2_words = [
             keep.tile([P, D], U32, name="w2_words%d" % g, align_bytes=64) for g in range(F_CHUNKS)
         ]
-        w1_planes = keep.tile([P, F], U8, name="w1_planes", align_bytes=64)
+        w1_planes = [
+            keep.tile([P, F // 2], U8, name="w1_planes%d" % x, align_bytes=64) for x in range(2)
+        ]
         w2_planes = [
             keep.tile([P, D], U8, name="w2_planes%d" % j, align_bytes=64)
             for j in range(F_CHUNKS // PLANES_PER_TILE)
@@ -84,10 +85,9 @@ def tile_ffnn_encoder_pc_kernel(
         eps = keep.tile([P, 1], F32, name="eps")
         first_sqrt = keep.tile([P, 1], F32, name="first_sqrt")
 
-        nc.vector.memset(bias_rows[:], 0.0)
-        nc.vector.memset(w1_planes[:].bitcast(I32), 0)
+        nc.gpsimd.memset(bias_rows[:], 0.0)
         nc.vector.memset(eps[:], EPS)
-        for plane_tile in w2_planes:
+        for plane_tile in w1_planes + w2_planes:
             nc.vector.memset(plane_tile[:].bitcast(I32), 0)
         make_identity(nc, ident_bf16[:])
         make_identity(nc, ident_f32[:])
@@ -118,9 +118,10 @@ def tile_ffnn_encoder_pc_kernel(
         )
         for m in range(TOK_TILES):
             load_h(m)
-        load_planes(w1_planes, W1_scales)
-        for g in range(F_CHUNKS):
-            load_w1_chunk(g)
+        for x in range(2):
+            load_planes(w1_planes[x], W1_scales[:, :, (F // 2) * x : (F // 2) * (x + 1)])
+            for g in range(4 * x, 4 * (x + 1)):
+                load_w1_chunk(g)
         for j in range(F_CHUNKS // PLANES_PER_TILE):
             load_planes(w2_planes[j], W2_scales[PLANES_PER_TILE * j : PLANES_PER_TILE * (j + 1)])
         for g in range(F_CHUNKS):
@@ -148,30 +149,25 @@ def tile_ffnn_encoder_pc_kernel(
             )
             return bank
 
-        def broadcast_b1(g):
-            bank = broadcast_row(g)
-            nc.scalar.copy(out=sorted_view(b1_sorted[g][:]), in_=natural_as_sorted(bank[:]))
-
-        def broadcast_b2(half):
-            bank = broadcast_row(F_CHUNKS + half)
-            nc.scalar.copy(out=b2_bc[:, half * N_TILE : (half + 1) * N_TILE], in_=bank[:])
-
-        def sort_h(m):
-            nc.vector.tensor_copy(
-                out=x_sorted[m][:].bitcast(F32).rearrange("p (c u q) -> p c u q", c=D_PASSES, u=2),
-                in_=x_sb[m][:].bitcast(F32).rearrange("p (c q u) -> p c u q", c=D_PASSES, u=2),
-            )
+        def broadcast_bias(row):
+            bank = broadcast_row(row)
+            if row < F_CHUNKS:
+                nc.scalar.copy(out=sorted_view(b1_sorted[row][:]), in_=natural_as_sorted(bank[:]))
+            else:
+                half = row - F_CHUNKS
+                nc.scalar.copy(out=b2_bc[:, half * N_TILE : (half + 1) * N_TILE], in_=bank[:])
 
         h_grouped_tiles = {}
 
         def transpose_h(m):
-            x_as_words = x_sorted[m][:].bitcast(F32)
+            x_as_words = x_sb[m][:].bitcast(F32)
             bank = psum.tile([P, D_PASSES, 2, P], F32, tag="bank", name="hT_bank")
             for c in range(D_PASSES):
                 for u in range(2):
-                    plane = 2 * c + u
                     nc.tensor.transpose(
-                        bank[:, c, u, :], x_as_words[:, plane * P : (plane + 1) * P], ident_f32[:]
+                        bank[:, c, u, :],
+                        x_as_words[:, 256 * c + u : 256 * (c + 1) : 2],
+                        ident_f32[:],
                     )
             grouped = stream.tile([P, 4 * D_PASSES * P], BF16, name="h_grouped", align_bytes=64)
             h_grouped_tiles[m] = grouped
@@ -201,7 +197,9 @@ def tile_ffnn_encoder_pc_kernel(
                         lhsT=hq_words[m][:, c * P : (c + 1) * P].bitcast(FP8X4),
                         lhsT_scale=hq_scales[m][:, c * P : (c + 1) * P],
                         rhs=w1_words[g][:, c, :].bitcast(FP8X4),
-                        rhs_scale=w1_planes[4 * c : P, g * N_TILE : (g + 1) * N_TILE],
+                        rhs_scale=w1_planes[g // 4][
+                            4 * c : P, (g % 4) * N_TILE : (g % 4 + 1) * N_TILE
+                        ],
                         start=(c == 0),
                         stop=(c == D_PASSES - 1),
                     )
@@ -221,9 +219,11 @@ def tile_ffnn_encoder_pc_kernel(
 
         def transpose_hid(g):
             hid = hid_tiles[g]
-            grouped = stream.tile([P, 4 * TOKENS], BF16, name="hid_grouped", align_bytes=64)
-            grouped_tiles[g] = grouped
             for pair in range(TOK_TILES // 2):
+                grouped = stream.tile(
+                    [P, 4 * 2 * P], BF16, name="hid_grouped%d" % pair, align_bytes=64
+                )
+                grouped_tiles[(g, pair)] = grouped
                 bank = psum.tile([P, 2, 2 * P], F32, tag="bank", name="hidT_bank")
                 for i in range(2):
                     hid_as_words = hid[:, 2 * pair + i, :].bitcast(F32)
@@ -234,19 +234,19 @@ def tile_ffnn_encoder_pc_kernel(
                             ident_f32[:],
                         )
                 nc.scalar.activation(
-                    out=grouped[:, 8 * P * pair : 8 * P * (pair + 1)].rearrange(
-                        "p (w u e) -> p w u e", u=2, e=2
-                    ),
+                    out=grouped[:].rearrange("p (w u e) -> p w u e", u=2, e=2),
                     in_=bank[:].bitcast(BF16).rearrange("p u (w e) -> p w u e", e=2),
                     func=ACT.Relu,
                 )
 
         def quantise_hid(g):
-            nc.vector.quantize_mx(
-                out=hidq_words[g][:].bitcast(FP8X4),
-                scales=hidq_scales[g][:],
-                in_=grouped_tiles[g][:],
-            )
+            for pair in range(TOK_TILES // 2):
+                cols = slice(2 * P * pair, 2 * P * (pair + 1))
+                nc.vector.quantize_mx(
+                    out=hidq_words[g][:, cols].bitcast(FP8X4),
+                    scales=hidq_scales[g][:, cols],
+                    in_=grouped_tiles[(g, pair)][:],
+                )
 
         def residual(m, half):
             cols = slice(half * N_TILE, (half + 1) * N_TILE)
@@ -254,12 +254,14 @@ def tile_ffnn_encoder_pc_kernel(
                 out=res[m][:, cols], in0=x_sb[m][:, cols], in1=b2_bc[:, cols], op=ADD
             )
 
-        def second_matmul(m):
-            accs = [
+        def open_out_banks():
+            return [
                 psum.tile([P, N_TILE], F32, tag="bank", name="out_acc%d" % half)
                 for half in range(D_HALVES)
             ]
-            for g in range(F_CHUNKS):
+
+        def second_matmul(m, accs, chunks):
+            for g in chunks:
                 for half in range(D_HALVES):
                     offset = 4 * (g % PLANES_PER_TILE)
                     nc.tensor.matmul_mx(
@@ -273,7 +275,6 @@ def tile_ffnn_encoder_pc_kernel(
                         start=(g == 0),
                         stop=(g == F_CHUNKS - 1),
                     )
-            return accs
 
         def layer_norm(m, accs):
             r = norm.tile([P, D], F32, name="r")
@@ -326,27 +327,33 @@ def tile_ffnn_encoder_pc_kernel(
                 )
                 nc.sync.dma_start(out=out_rows[m * P : (m + 1) * P, cols], in_=result[:, cols])
 
-        for g in range(F_CHUNKS):
-            broadcast_b1(g)
-        for half in range(D_HALVES):
-            broadcast_b2(half)
+        broadcast_bias(0)
+        broadcast_bias(1)
         for m in range(TOK_TILES):
-            sort_h(m)
-        for step in range(TOK_TILES + 1):
-            if step < TOK_TILES:
-                transpose_h(step)
-            if 0 <= step - 1:
-                quantise_h(step - 1)
+            transpose_h(m)
+            broadcast_bias(2 * m + 2)
+            broadcast_bias(2 * m + 3)
+            if m >= 1:
+                quantise_h(m - 1)
+        quantise_h(TOK_TILES - 1)
 
-        for step in range(F_CHUNKS + 2):
-            if step < F_CHUNKS:
-                first_matmul(step)
-                residual(step // D_HALVES, step % D_HALVES)
-            if 0 <= step - 1 < F_CHUNKS:
+        for step in range(F_CHUNKS):
+            first_matmul(step)
+            residual(step // D_HALVES, step % D_HALVES)
+            if step >= 1:
                 transpose_hid(step - 1)
-            if 0 <= step - 2:
+            if step >= 2:
                 quantise_hid(step - 2)
 
-        for m in range(TOK_TILES):
-            accs = second_matmul(m)
+        EARLY_CHUNKS = 3
+        accs = open_out_banks()
+        second_matmul(0, accs, range(EARLY_CHUNKS))
+        transpose_hid(F_CHUNKS - 1)
+        quantise_hid(F_CHUNKS - 2)
+        quantise_hid(F_CHUNKS - 1)
+        second_matmul(0, accs, range(EARLY_CHUNKS, F_CHUNKS))
+        layer_norm(0, accs)
+        for m in range(1, TOK_TILES):
+            accs = open_out_banks()
+            second_matmul(m, accs, range(F_CHUNKS))
             layer_norm(m, accs)

@@ -203,19 +203,12 @@ def tile_ffnn_encoder_pc_kernel(
                         start=(c == 0),
                         stop=(c == D_PASSES - 1),
                     )
-                if m < TOK_TILES - 1:
-                    nc.vector.tensor_tensor(
-                        out=sorted_view(hid[:, m, :]),
-                        in0=natural_as_sorted(acc[:]),
-                        in1=sorted_view(b1_sorted[g][:]),
-                        op=ADD,
-                    )
-                else:
-                    raw = stream.tile([P, K_PASS], F32, name="hid_raw")
-                    nc.scalar.copy(out=sorted_view(raw[:]), in_=natural_as_sorted(acc[:]))
-                    nc.gpsimd.tensor_tensor(
-                        out=hid[:, m, :], in0=raw[:], in1=b1_sorted[g][:], op=ADD
-                    )
+                nc.vector.tensor_tensor(
+                    out=sorted_view(hid[:, m, :]),
+                    in0=natural_as_sorted(acc[:]),
+                    in1=sorted_view(b1_sorted[g][:]),
+                    op=ADD,
+                )
 
         def transpose_hid(g):
             hid = hid_tiles[g]

@@ -25,6 +25,7 @@ D_PASSES = D // K_PASS
 F_CHUNKS = F // K_PASS
 D_HALVES = D // N_TILE
 PLANES_PER_TILE = 4
+PACK = 4
 
 FLOPS = 2 * TOKENS * D * F * 2
 
@@ -41,9 +42,14 @@ def tile_ffnn_encoder_pc_kernel(
         keep = ctx.enter_context(tc.tile_pool(name="keep", bufs=1))
         stream = ctx.enter_context(tc.tile_pool(name="stream", bufs=3))
         norm = ctx.enter_context(tc.tile_pool(name="norm", bufs=2))
-        psum = ctx.enter_context(tc.psum_pool(name="psum", bufs=8))
+        psum_a = ctx.enter_context(tc.psum_pool(name="psum_a", bufs=6))
+        psum_o = ctx.enter_context(tc.psum_pool(name="psum_o", bufs=2))
 
         x_sb = [keep.tile([P, D], BF16, name="x_sb%d" % m) for m in range(TOK_TILES)]
+        w1_raw = [
+            keep.tile([P, D_PASSES, N_TILE], U32, name="w1_raw%d" % g, align_bytes=64)
+            for g in range(F_CHUNKS)
+        ]
         w1_words = [
             keep.tile([P, D_PASSES, N_TILE], U32, name="w1_words%d" % g, align_bytes=64)
             for g in range(F_CHUNKS)
@@ -51,20 +57,25 @@ def tile_ffnn_encoder_pc_kernel(
         w2_words = [
             keep.tile([P, D], U32, name="w2_words%d" % g, align_bytes=64) for g in range(F_CHUNKS)
         ]
+        w1_raw_planes = keep.tile([P, F // 2], U8, name="w1_raw_planes", align_bytes=64)
         w1_planes = [
-            keep.tile([P, F // 2], U8, name="w1_planes%d" % x, align_bytes=64) for x in range(2)
+            keep.tile([P, K_PASS], U8, name="w1_planes%d" % q, align_bytes=64) for q in range(4)
         ]
         w2_planes = [
             keep.tile([P, D], U8, name="w2_planes%d" % j, align_bytes=64)
             for j in range(F_CHUNKS // PLANES_PER_TILE)
         ]
+        h_grouped = [
+            keep.tile([P, D_PASSES, 2 * P, PACK], BF16, name="h_grouped%d" % i, align_bytes=64)
+            for i in range(2)
+        ]
         hq_words = [
-            keep.tile([P, D_PASSES * P], U32, name="hq_words%d" % m, align_bytes=64)
-            for m in range(TOK_TILES)
+            keep.tile([P, TOKENS], U32, name="hq_words%d" % c, align_bytes=64)
+            for c in range(D_PASSES)
         ]
         hq_scales = [
-            keep.tile([P, D_PASSES * P], U8, name="hq_scales%d" % m, align_bytes=64)
-            for m in range(TOK_TILES)
+            keep.tile([P, TOKENS], U8, name="hq_scales%d" % c, align_bytes=64)
+            for c in range(D_PASSES)
         ]
         hidq_words = [
             keep.tile([P, TOKENS], U32, name="hidq_words%d" % g, align_bytes=64)
@@ -74,8 +85,8 @@ def tile_ffnn_encoder_pc_kernel(
             keep.tile([P, TOKENS], U8, name="hidq_scales%d" % g, align_bytes=64)
             for g in range(F_CHUNKS)
         ]
-        b1_sorted = [keep.tile([P, K_PASS], BF16, name="b1_sorted%d" % g) for g in range(F_CHUNKS)]
         bias_rows = keep.tile([P, N_TILE], BF16, name="bias_rows")
+        b1_cols = keep.tile([P, PACK, F_CHUNKS], F32, name="b1_cols")
         res = [keep.tile([P, D], F32, name="res%d" % m) for m in range(TOK_TILES)]
         b2_bc = keep.tile([P, D], BF16, name="b2_bc")
         g2_bc = keep.tile([P, D], BF16, name="g2_bc")
@@ -87,27 +98,32 @@ def tile_ffnn_encoder_pc_kernel(
 
         nc.gpsimd.memset(bias_rows[:], 0.0)
         nc.vector.memset(eps[:], EPS)
-        for plane_tile in w1_planes + w2_planes:
+        nc.vector.memset(w1_raw_planes[:].bitcast(I32), 0)
+        for plane_tile in w2_planes:
             nc.vector.memset(plane_tile[:].bitcast(I32), 0)
         make_identity(nc, ident_bf16[:])
         make_identity(nc, ident_f32[:])
         nc.scalar.activation(out=first_sqrt[:], in_=eps[:], func=ACT.Sqrt)
 
-        def load_h(m):
-            nc.sync.dma_start(out=x_sb[m][:], in_=h_rows[m * P : (m + 1) * P, :])
-
         def load_w1_chunk(g):
             by_partition = W1_words.rearrange("c p n t -> p c (n t)")
             nc.sync.dma_start(
-                out=w1_words[g][:].bitcast(I32),
+                out=w1_raw[g][:].bitcast(I32),
                 in_=by_partition[:, :, 4 * N_TILE * g : 4 * N_TILE * (g + 1)].bitcast(I32),
             )
 
-        def load_planes(plane_tile, scales):
+        def load_w2_chunk(g):
+            nc.sync.dma_start(
+                out=w2_words[g][:].bitcast(I32),
+                in_=W2_words[g].rearrange("p n t -> p (n t)").bitcast(I32),
+            )
+
+        def load_planes(plane_tile, first, scales):
             n_planes = scales.shape[0]
             for quadrant in range(4):
+                row = 32 * quadrant + 4 * first
                 nc.sync.dma_start(
-                    out=plane_tile[32 * quadrant : 32 * quadrant + 4 * n_planes, :].bitcast(I32),
+                    out=plane_tile[row : row + 4 * n_planes, :].bitcast(I32),
                     in_=scales[:, 4 * quadrant : 4 * quadrant + 4, :].bitcast(I32),
                 )
 
@@ -117,29 +133,33 @@ def tile_ffnn_encoder_pc_kernel(
             in_=b2.rearrange("(r c) -> r c", c=N_TILE),
         )
         for m in range(TOK_TILES):
-            load_h(m)
+            nc.sync.dma_start(out=x_sb[m][:], in_=h_rows[m * P : (m + 1) * P, :])
         for x in range(2):
-            load_planes(w1_planes[x], W1_scales[:, :, (F // 2) * x : (F // 2) * (x + 1)])
-            for g in range(4 * x, 4 * (x + 1)):
-                load_w1_chunk(g)
-        for j in range(F_CHUNKS // PLANES_PER_TILE):
-            load_planes(w2_planes[j], W2_scales[PLANES_PER_TILE * j : PLANES_PER_TILE * (j + 1)])
-        for g in range(F_CHUNKS):
-            nc.sync.dma_start(
-                out=w2_words[g][:].bitcast(I32),
-                in_=W2_words[g].rearrange("p n t -> p (n t)").bitcast(I32),
+            load_planes(
+                w1_raw_planes, D_PASSES * x, W1_scales[:, :, (F // 2) * x : (F // 2) * (x + 1)]
             )
+        for g in range(4):
+            load_w1_chunk(g)
+        for j in range(F_CHUNKS // PLANES_PER_TILE):
+            load_planes(w2_planes[j], 0, W2_scales[PLANES_PER_TILE * j : PLANES_PER_TILE * (j + 1)])
+        for g in range(4):
+            load_w2_chunk(g)
+            load_w1_chunk(g + 4)
+        for g in range(4, F_CHUNKS):
+            load_w2_chunk(g)
         nc.sync.dma_start(out=g2_bc[:], in_=g2.partition_broadcast(P))
         nc.sync.dma_start(out=beta2_bc[:], in_=beta2.partition_broadcast(P))
 
-        def sorted_view(ap):
-            return ap.rearrange("p (u q e) -> p u q e", u=2, e=2)
+        def b1_to_partitions():
+            bank = psum_a.tile([P, 2 * PACK, P], BF16, tag="bank", name="b1_bank")
+            by_slot = bias_rows[:].rearrange("r (p t) -> r t p", t=PACK)
+            for t in range(PACK):
+                nc.tensor.transpose(bank[:, t, :], by_slot[:, t, :], ident_bf16[:])
+            nc.scalar.copy(out=b1_cols[:], in_=bank[:, 0:PACK, 0:F_CHUNKS])
 
-        def natural_as_sorted(ap):
-            return ap.rearrange("p (q u e) -> p u q e", u=2, e=2)
-
-        def broadcast_row(row):
-            bank = psum.tile([P, N_TILE], F32, tag="bank", name="bias_bank")
+        def broadcast_b2(half):
+            row = F_CHUNKS + half
+            bank = psum_a.tile([P, N_TILE], F32, tag="bank", name="b2_bank")
             nc.tensor.matmul(
                 out=bank[:],
                 lhsT=ident_bf16[:, row : row + 1].to_broadcast([P, P]),
@@ -147,21 +167,11 @@ def tile_ffnn_encoder_pc_kernel(
                 start=True,
                 stop=True,
             )
-            return bank
-
-        def broadcast_bias(row):
-            bank = broadcast_row(row)
-            if row < F_CHUNKS:
-                nc.scalar.copy(out=sorted_view(b1_sorted[row][:]), in_=natural_as_sorted(bank[:]))
-            else:
-                half = row - F_CHUNKS
-                nc.scalar.copy(out=b2_bc[:, half * N_TILE : (half + 1) * N_TILE], in_=bank[:])
-
-        h_grouped_tiles = {}
+            nc.scalar.copy(out=b2_bc[:, half * N_TILE : (half + 1) * N_TILE], in_=bank[:])
 
         def transpose_h(m):
             x_as_words = x_sb[m][:].bitcast(F32)
-            bank = psum.tile([P, D_PASSES, 2, P], F32, tag="bank", name="hT_bank")
+            bank = psum_a.tile([P, D_PASSES, 2, P], F32, tag="bank", name="hT_bank")
             for c in range(D_PASSES):
                 for u in range(2):
                     nc.tensor.transpose(
@@ -169,77 +179,74 @@ def tile_ffnn_encoder_pc_kernel(
                         x_as_words[:, 256 * c + u : 256 * (c + 1) : 2],
                         ident_f32[:],
                     )
-            grouped = stream.tile([P, 4 * D_PASSES * P], BF16, name="h_grouped", align_bytes=64)
-            h_grouped_tiles[m] = grouped
+            tokens = slice((m % 2) * P, (m % 2 + 1) * P)
+            words = h_grouped[m // 2][:].rearrange("p c n k -> p (c n k)").bitcast(F32)
+            words = words.rearrange("p (c n u) -> p c n u", c=D_PASSES, u=2)
+            copy = nc.vector.tensor_copy if m % 2 == 0 else nc.scalar.copy
+            copy(out=words[:, :, tokens, :], in_=bank[:].rearrange("p c u n -> p c n u"))
+
+        def quantise_h(i):
+            cols = slice(2 * P * i, 2 * P * (i + 1))
+            for c in range(D_PASSES):
+                nc.vector.quantize_mx(
+                    out=hq_words[c][:, cols].bitcast(FP8X4),
+                    scales=hq_scales[c][:, cols],
+                    in_=h_grouped[i][:, c, :, :].rearrange("p n k -> p (n k)"),
+                )
+
+        def permute_planes(q):
             nc.vector.tensor_copy(
-                out=grouped[:].bitcast(F32).rearrange("p (c w u) -> p c w u", c=D_PASSES, u=2),
-                in_=bank[:].rearrange("p c u w -> p c w u"),
+                out=w1_planes[q][:].rearrange("p (t m) -> p m t", t=PACK),
+                in_=w1_raw_planes[:, K_PASS * q : K_PASS * (q + 1)].rearrange(
+                    "p (m t) -> p m t", t=PACK
+                ),
             )
 
-        def quantise_h(m):
-            nc.vector.quantize_mx(
-                out=hq_words[m][:].bitcast(FP8X4),
-                scales=hq_scales[m][:],
-                in_=h_grouped_tiles[m][:],
+        def permute_words(g):
+            nc.vector.tensor_copy(
+                out=w1_words[g][:].bitcast(I32).rearrange("p c (t m) -> p c t m", t=PACK),
+                in_=w1_raw[g][:].bitcast(I32).rearrange("p c (m t) -> p c t m", t=PACK),
             )
 
         hid_tiles = {}
         grouped_tiles = {}
 
         def first_matmul(g):
-            hid = stream.tile([P, TOK_TILES, K_PASS], BF16, name="hid")
+            hid = stream.tile([P, PACK, TOKENS], BF16, name="hid")
             hid_tiles[g] = hid
-            for m in range(TOK_TILES):
-                acc = psum.tile([P, N_TILE], F32, tag="bank", name="hid_acc")
+            x, q = divmod(g, 4)
+            for t in range(PACK):
+                acc = psum_a.tile([P, TOKENS], F32, tag="bank", name="hid_acc")
+                cols = slice(t * P, (t + 1) * P)
                 for c in range(D_PASSES):
                     nc.tensor.matmul_mx(
                         out=acc[:],
-                        lhsT=hq_words[m][:, c * P : (c + 1) * P].bitcast(FP8X4),
-                        lhsT_scale=hq_scales[m][:, c * P : (c + 1) * P],
-                        rhs=w1_words[g][:, c, :].bitcast(FP8X4),
-                        rhs_scale=w1_planes[g // 4][
-                            4 * c : P, (g % 4) * N_TILE : (g % 4 + 1) * N_TILE
-                        ],
+                        lhsT=w1_words[g][:, c, cols].bitcast(FP8X4),
+                        lhsT_scale=w1_planes[q][4 * (D_PASSES * x + c) : P, cols],
+                        rhs=hq_words[c][:].bitcast(FP8X4),
+                        rhs_scale=hq_scales[c][:],
                         start=(c == 0),
                         stop=(c == D_PASSES - 1),
                     )
-                nc.vector.tensor_tensor(
-                    out=sorted_view(hid[:, m, :]),
-                    in0=natural_as_sorted(acc[:]),
-                    in1=sorted_view(b1_sorted[g][:]),
-                    op=ADD,
+                nc.scalar.activation(
+                    out=hid[:, t, :], in_=acc[:], func=ACT.Relu, bias=b1_cols[:, t, g : g + 1]
                 )
 
-        def transpose_hid(g):
-            hid = hid_tiles[g]
-            for pair in range(TOK_TILES // 2):
-                grouped = stream.tile(
-                    [P, 4 * 2 * P], BF16, name="hid_grouped%d" % pair, align_bytes=64
-                )
-                grouped_tiles[(g, pair)] = grouped
-                bank = psum.tile([P, 2, 2 * P], F32, tag="bank", name="hidT_bank")
-                for i in range(2):
-                    hid_as_words = hid[:, 2 * pair + i, :].bitcast(F32)
-                    for u in range(2):
-                        nc.tensor.transpose(
-                            bank[:, u, i * P : (i + 1) * P],
-                            hid_as_words[:, u * P : (u + 1) * P],
-                            ident_f32[:],
-                        )
-                nc.scalar.activation(
-                    out=grouped[:].rearrange("p (w u e) -> p w u e", u=2, e=2),
-                    in_=bank[:].bitcast(BF16).rearrange("p u (w e) -> p w u e", e=2),
-                    func=ACT.Relu,
+        def interleave(g):
+            grouped = stream.tile([P, TOKENS, PACK], BF16, name="hid_grouped", align_bytes=64)
+            grouped_tiles[g] = grouped
+            for i in range(2):
+                cols = slice(i * 2 * P, (i + 1) * 2 * P)
+                nc.vector.tensor_copy(
+                    out=grouped[:, cols, :], in_=hid_tiles[g][:, :, cols].rearrange("p t n -> p n t")
                 )
 
         def quantise_hid(g):
-            for pair in range(TOK_TILES // 2):
-                cols = slice(2 * P * pair, 2 * P * (pair + 1))
-                nc.vector.quantize_mx(
-                    out=hidq_words[g][:, cols].bitcast(FP8X4),
-                    scales=hidq_scales[g][:, cols],
-                    in_=grouped_tiles[(g, pair)][:],
-                )
+            nc.vector.quantize_mx(
+                out=hidq_words[g][:].bitcast(FP8X4),
+                scales=hidq_scales[g][:],
+                in_=grouped_tiles[g][:].rearrange("p n t -> p (n t)"),
+            )
 
         def residual(m, half):
             cols = slice(half * N_TILE, (half + 1) * N_TILE)
@@ -247,24 +254,23 @@ def tile_ffnn_encoder_pc_kernel(
                 out=res[m][:, cols], in0=x_sb[m][:, cols], in1=b2_bc[:, cols], op=ADD
             )
 
-        def open_out_banks():
+        def open_out_banks(pool):
             return [
-                psum.tile([P, N_TILE], F32, tag="bank", name="out_acc%d" % half)
+                pool.tile([P, N_TILE], F32, tag="bank", name="out_acc%d" % half)
                 for half in range(D_HALVES)
             ]
 
-        def second_matmul(m, accs, chunks):
+        def second_matmul(m, accs, chunks, halves=(0, 1)):
             for g in chunks:
-                for half in range(D_HALVES):
+                for half in halves:
                     offset = 4 * (g % PLANES_PER_TILE)
+                    cols = slice(half * N_TILE, (half + 1) * N_TILE)
                     nc.tensor.matmul_mx(
                         out=accs[half][:],
                         lhsT=hidq_words[g][:, m * P : (m + 1) * P].bitcast(FP8X4),
                         lhsT_scale=hidq_scales[g][:, m * P : (m + 1) * P],
-                        rhs=w2_words[g][:, half * N_TILE : (half + 1) * N_TILE].bitcast(FP8X4),
-                        rhs_scale=w2_planes[g // PLANES_PER_TILE][
-                            offset:P, half * N_TILE : (half + 1) * N_TILE
-                        ],
+                        rhs=w2_words[g][:, cols].bitcast(FP8X4),
+                        rhs_scale=w2_planes[g // PLANES_PER_TILE][offset:P, cols],
                         start=(g == 0),
                         stop=(g == F_CHUNKS - 1),
                     )
@@ -320,33 +326,44 @@ def tile_ffnn_encoder_pc_kernel(
                 )
                 nc.sync.dma_start(out=out_rows[m * P : (m + 1) * P, cols], in_=result[:, cols])
 
-        broadcast_bias(0)
-        broadcast_bias(1)
+        b1_to_partitions()
+        broadcast_b2(0)
+        broadcast_b2(1)
         for m in range(TOK_TILES):
             transpose_h(m)
-            broadcast_bias(2 * m + 2)
-            broadcast_bias(2 * m + 3)
-            if m >= 1:
-                quantise_h(m - 1)
-        quantise_h(TOK_TILES - 1)
+            residual(m, 0)
+            residual(m, 1)
+            if m % 2 == 1:
+                quantise_h(m // 2)
+        permute_planes(0)
+        permute_words(0)
+        permute_planes(1)
+        permute_words(1)
 
-        for step in range(F_CHUNKS):
-            first_matmul(step)
-            residual(step // D_HALVES, step % D_HALVES)
-            if step >= 1:
-                transpose_hid(step - 1)
-            if step >= 2:
-                quantise_hid(step - 2)
+        accs = {0: open_out_banks(psum_o)}
+        for g in range(F_CHUNKS):
+            first_matmul(g)
+            if g >= 1:
+                interleave(g - 1)
+            if g + 2 < F_CHUNKS:
+                if g + 2 < 4:
+                    permute_planes(g + 2)
+                permute_words(g + 2)
+            if g >= 1:
+                quantise_hid(g - 1)
+            if g >= 2:
+                second_matmul(0, accs[0], [g - 2])
 
-        EARLY_CHUNKS = 3
-        accs = open_out_banks()
-        second_matmul(0, accs, range(EARLY_CHUNKS))
-        transpose_hid(F_CHUNKS - 1)
-        quantise_hid(F_CHUNKS - 2)
-        quantise_hid(F_CHUNKS - 1)
-        second_matmul(0, accs, range(EARLY_CHUNKS, F_CHUNKS))
-        layer_norm(0, accs)
-        for m in range(1, TOK_TILES):
-            accs = open_out_banks()
-            second_matmul(m, accs, range(F_CHUNKS))
-            layer_norm(m, accs)
+        last = F_CHUNKS - 1
+        accs[1] = open_out_banks(psum_a)
+        second_matmul(1, accs[1], range(last))
+        interleave(last)
+        quantise_hid(last)
+        second_matmul(0, accs[0], [last - 1, last])
+        layer_norm(0, accs[0])
+        second_matmul(1, accs[1], [last])
+        layer_norm(1, accs[1])
+        for m in range(2, TOK_TILES):
+            accs[m] = open_out_banks(psum_a)
+            second_matmul(m, accs[m], range(F_CHUNKS))
+            layer_norm(m, accs[m])

@@ -26,6 +26,7 @@ F_CHUNKS = F // K_PASS
 D_HALVES = D // N_TILE
 PLANES_PER_TILE = 4
 PACK = 4
+HALF = TOKENS // 2
 
 FLOPS = 2 * TOKENS * D * F * 2
 
@@ -57,16 +58,17 @@ def tile_ffnn_encoder_pc_kernel(
         w2_words = [
             keep.tile([P, D], U32, name="w2_words%d" % g, align_bytes=64) for g in range(F_CHUNKS)
         ]
-        w1_raw_planes = keep.tile([P, F // 2], U8, name="w1_raw_planes", align_bytes=64)
+        w1_raw_planes = keep.tile([P, D_PASSES, 2 * K_PASS], U8, name="w1_raw_planes", align_bytes=64)
         w1_planes = [
-            keep.tile([P, K_PASS], U8, name="w1_planes%d" % q, align_bytes=64) for q in range(4)
+            keep.tile([P, D_PASSES * K_PASS], U8, name="w1_planes%d" % q, align_bytes=64)
+            for q in range(2)
         ]
         w2_planes = [
             keep.tile([P, D], U8, name="w2_planes%d" % j, align_bytes=64)
             for j in range(F_CHUNKS // PLANES_PER_TILE)
         ]
         h_grouped = [
-            keep.tile([P, D_PASSES, 2 * P, PACK], BF16, name="h_grouped%d" % i, align_bytes=64)
+            keep.tile([P, D_PASSES, HALF, PACK], BF16, name="h_grouped%d" % i, align_bytes=64)
             for i in range(2)
         ]
         hq_words = [
@@ -98,12 +100,15 @@ def tile_ffnn_encoder_pc_kernel(
 
         nc.gpsimd.memset(bias_rows[:], 0.0)
         nc.vector.memset(eps[:], EPS)
-        nc.vector.memset(w1_raw_planes[:].bitcast(I32), 0)
+        nc.vector.memset(w1_raw_planes[:].rearrange("p c n -> p (c n)").bitcast(I32), 0)
         for plane_tile in w2_planes:
             nc.vector.memset(plane_tile[:].bitcast(I32), 0)
         make_identity(nc, ident_bf16[:])
         make_identity(nc, ident_f32[:])
         nc.scalar.activation(out=first_sqrt[:], in_=eps[:], func=ACT.Sqrt)
+
+        def load_h(m):
+            nc.sync.dma_start(out=x_sb[m][:], in_=h_rows[m * P : (m + 1) * P, :])
 
         def load_w1_chunk(g):
             by_partition = W1_words.rearrange("c p n t -> p c (n t)")
@@ -118,35 +123,40 @@ def tile_ffnn_encoder_pc_kernel(
                 in_=W2_words[g].rearrange("p n t -> p (n t)").bitcast(I32),
             )
 
-        def load_planes(plane_tile, first, scales):
-            n_planes = scales.shape[0]
-            for quadrant in range(4):
-                row = 32 * quadrant + 4 * first
+        def load_w1_planes(c, quadrants):
+            for quadrant in quadrants:
+                rows = W1_scales[c, 4 * quadrant : 4 * quadrant + 4, :]
                 nc.sync.dma_start(
-                    out=plane_tile[row : row + 4 * n_planes, :].bitcast(I32),
+                    out=w1_raw_planes[32 * quadrant : 32 * quadrant + 16, c, :].bitcast(I32),
+                    in_=rows.rearrange("r (x n) -> x r n", n=2 * K_PASS).bitcast(I32),
+                )
+
+        def load_w2_planes(j):
+            scales = W2_scales[PLANES_PER_TILE * j : PLANES_PER_TILE * (j + 1)]
+            for quadrant in range(4):
+                nc.sync.dma_start(
+                    out=w2_planes[j][32 * quadrant : 32 * quadrant + 16, :].bitcast(I32),
                     in_=scales[:, 4 * quadrant : 4 * quadrant + 4, :].bitcast(I32),
                 )
 
+        load_w1_planes(0, range(4))
+        for m in range(TOK_TILES):
+            load_h(m)
+        load_w1_planes(1, range(4))
+        load_w1_chunk(0)
         nc.sync.dma_start(out=bias_rows[0:F_CHUNKS, :], in_=b1.rearrange("(r c) -> r c", c=N_TILE))
         nc.sync.dma_start(
             out=bias_rows[F_CHUNKS : F_CHUNKS + D_HALVES, :],
             in_=b2.rearrange("(r c) -> r c", c=N_TILE),
         )
-        for m in range(TOK_TILES):
-            nc.sync.dma_start(out=x_sb[m][:], in_=h_rows[m * P : (m + 1) * P, :])
-        for x in range(2):
-            load_planes(
-                w1_raw_planes, D_PASSES * x, W1_scales[:, :, (F // 2) * x : (F // 2) * (x + 1)]
-            )
-        for g in range(4):
+        for g in range(1, 4):
             load_w1_chunk(g)
-        for j in range(F_CHUNKS // PLANES_PER_TILE):
-            load_planes(w2_planes[j], 0, W2_scales[PLANES_PER_TILE * j : PLANES_PER_TILE * (j + 1)])
-        for g in range(4):
+        load_w2_planes(0)
+        load_w2_planes(1)
+        for g in range(F_CHUNKS):
             load_w2_chunk(g)
-            load_w1_chunk(g + 4)
-        for g in range(4, F_CHUNKS):
-            load_w2_chunk(g)
+            if g + 4 < F_CHUNKS:
+                load_w1_chunk(g + 4)
         nc.sync.dma_start(out=g2_bc[:], in_=g2.partition_broadcast(P))
         nc.sync.dma_start(out=beta2_bc[:], in_=beta2.partition_broadcast(P))
 
@@ -157,17 +167,35 @@ def tile_ffnn_encoder_pc_kernel(
                 nc.tensor.transpose(bank[:, t, :], by_slot[:, t, :], ident_bf16[:])
             nc.scalar.copy(out=b1_cols[:], in_=bank[:, 0:PACK, 0:F_CHUNKS])
 
-        def broadcast_b2(half):
+        def spread_b2(bank, half, start, stop):
             row = F_CHUNKS + half
-            bank = psum_a.tile([P, N_TILE], F32, tag="bank", name="b2_bank")
             nc.tensor.matmul(
                 out=bank[:],
                 lhsT=ident_bf16[:, row : row + 1].to_broadcast([P, P]),
                 rhs=bias_rows[:],
-                start=True,
-                stop=True,
+                start=start,
+                stop=stop,
             )
+
+        def broadcast_b2(half):
+            bank = psum_a.tile([P, N_TILE], F32, tag="bank", name="b2_bank")
+            spread_b2(bank, half, True, True)
             nc.scalar.copy(out=b2_bc[:, half * N_TILE : (half + 1) * N_TILE], in_=bank[:])
+
+        def residual_by_tensor(m, half):
+            cols = slice(half * N_TILE, (half + 1) * N_TILE)
+            bank = psum_o.tile([P, N_TILE], F32, tag="bank", name="res_bank")
+            nc.tensor.matmul(
+                out=bank[:], lhsT=ident_bf16[:], rhs=x_sb[m][:, cols], start=True, stop=False
+            )
+            spread_b2(bank, half, False, True)
+            nc.scalar.copy(out=res[m][:, cols], in_=bank[:])
+
+        def residual_by_vector(m, half):
+            cols = slice(half * N_TILE, (half + 1) * N_TILE)
+            nc.vector.tensor_tensor(
+                out=res[m][:, cols], in0=x_sb[m][:, cols], in1=b2_bc[:, cols], op=ADD
+            )
 
         def transpose_h(m):
             x_as_words = x_sb[m][:].bitcast(F32)
@@ -186,7 +214,7 @@ def tile_ffnn_encoder_pc_kernel(
             copy(out=words[:, :, tokens, :], in_=bank[:].rearrange("p c u n -> p c n u"))
 
         def quantise_h(i):
-            cols = slice(2 * P * i, 2 * P * (i + 1))
+            cols = slice(HALF * i, HALF * (i + 1))
             for c in range(D_PASSES):
                 nc.vector.quantize_mx(
                     out=hq_words[c][:, cols].bitcast(FP8X4),
@@ -194,10 +222,12 @@ def tile_ffnn_encoder_pc_kernel(
                     in_=h_grouped[i][:, c, :, :].rearrange("p n k -> p (n k)"),
                 )
 
-        def permute_planes(q):
+        def permute_planes(q, c):
             nc.vector.tensor_copy(
-                out=w1_planes[q][:].rearrange("p (t m) -> p m t", t=PACK),
-                in_=w1_raw_planes[:, K_PASS * q : K_PASS * (q + 1)].rearrange(
+                out=w1_planes[q][:, c * K_PASS : (c + 1) * K_PASS].rearrange(
+                    "p (t m) -> p m t", t=PACK
+                ),
+                in_=w1_raw_planes[:, c, K_PASS * q : K_PASS * (q + 1)].rearrange(
                     "p (m t) -> p m t", t=PACK
                 ),
             )
@@ -211,47 +241,47 @@ def tile_ffnn_encoder_pc_kernel(
         hid_tiles = {}
         grouped_tiles = {}
 
-        def first_matmul(g):
+        def first_matmul(g, pieces=1):
             hid = stream.tile([P, PACK, TOKENS], BF16, name="hid")
             hid_tiles[g] = hid
-            x, q = divmod(g, 4)
-            for t in range(PACK):
-                acc = psum_a.tile([P, TOKENS], F32, tag="bank", name="hid_acc")
-                cols = slice(t * P, (t + 1) * P)
-                for c in range(D_PASSES):
-                    nc.tensor.matmul_mx(
-                        out=acc[:],
-                        lhsT=w1_words[g][:, c, cols].bitcast(FP8X4),
-                        lhsT_scale=w1_planes[q][4 * (D_PASSES * x + c) : P, cols],
-                        rhs=hq_words[c][:].bitcast(FP8X4),
-                        rhs_scale=hq_scales[c][:],
-                        start=(c == 0),
-                        stop=(c == D_PASSES - 1),
+            x, q = divmod(g, 2)
+            width = TOKENS // pieces
+            for i in range(pieces):
+                tokens = slice(width * i, width * (i + 1))
+                for t in range(PACK):
+                    acc = psum_a.tile([P, width], F32, tag="bank", name="hid_acc")
+                    for c in range(D_PASSES):
+                        nc.tensor.matmul_mx(
+                            out=acc[:],
+                            lhsT=w1_words[g][:, c, t * P : (t + 1) * P].bitcast(FP8X4),
+                            lhsT_scale=w1_planes[q][
+                                4 * x : P, c * K_PASS + t * P : c * K_PASS + (t + 1) * P
+                            ],
+                            rhs=hq_words[c][:, tokens].bitcast(FP8X4),
+                            rhs_scale=hq_scales[c][:, tokens],
+                            start=(c == 0),
+                            stop=(c == D_PASSES - 1),
+                        )
+                    nc.scalar.activation(
+                        out=hid[:, t, tokens], in_=acc[:], func=ACT.Relu, bias=b1_cols[:, t, g : g + 1]
                     )
-                nc.scalar.activation(
-                    out=hid[:, t, :], in_=acc[:], func=ACT.Relu, bias=b1_cols[:, t, g : g + 1]
-                )
 
-        def interleave(g):
-            grouped = stream.tile([P, TOKENS, PACK], BF16, name="hid_grouped", align_bytes=64)
-            grouped_tiles[g] = grouped
-            for i in range(2):
-                cols = slice(i * 2 * P, (i + 1) * 2 * P)
-                nc.vector.tensor_copy(
-                    out=grouped[:, cols, :], in_=hid_tiles[g][:, :, cols].rearrange("p t n -> p n t")
+        def interleave(g, half):
+            if half == 0:
+                grouped_tiles[g] = stream.tile(
+                    [P, TOKENS, PACK], BF16, name="hid_grouped", align_bytes=64
                 )
-
-        def quantise_hid(g):
-            nc.vector.quantize_mx(
-                out=hidq_words[g][:].bitcast(FP8X4),
-                scales=hidq_scales[g][:],
-                in_=grouped_tiles[g][:].rearrange("p n t -> p (n t)"),
+            cols = slice(HALF * half, HALF * (half + 1))
+            nc.vector.tensor_copy(
+                out=grouped_tiles[g][:, cols, :], in_=hid_tiles[g][:, :, cols].rearrange("p t n -> p n t")
             )
 
-        def residual(m, half):
-            cols = slice(half * N_TILE, (half + 1) * N_TILE)
-            nc.gpsimd.tensor_tensor(
-                out=res[m][:, cols], in0=x_sb[m][:, cols], in1=b2_bc[:, cols], op=ADD
+        def quantise_hid(g, half):
+            cols = slice(HALF * half, HALF * (half + 1))
+            nc.vector.quantize_mx(
+                out=hidq_words[g][:, cols].bitcast(FP8X4),
+                scales=hidq_scales[g][:, cols],
+                in_=grouped_tiles[g][:, cols, :].rearrange("p n t -> p (n t)"),
             )
 
         def open_out_banks(pool):
@@ -261,14 +291,15 @@ def tile_ffnn_encoder_pc_kernel(
             ]
 
         def second_matmul(m, accs, chunks, halves=(0, 1)):
+            rows = slice(m * P, (m + 1) * P)
             for g in chunks:
                 for half in halves:
                     offset = 4 * (g % PLANES_PER_TILE)
                     cols = slice(half * N_TILE, (half + 1) * N_TILE)
                     nc.tensor.matmul_mx(
                         out=accs[half][:],
-                        lhsT=hidq_words[g][:, m * P : (m + 1) * P].bitcast(FP8X4),
-                        lhsT_scale=hidq_scales[g][:, m * P : (m + 1) * P],
+                        lhsT=hidq_words[g][:, rows].bitcast(FP8X4),
+                        lhsT_scale=hidq_scales[g][:, rows],
                         rhs=w2_words[g][:, cols].bitcast(FP8X4),
                         rhs_scale=w2_planes[g // PLANES_PER_TILE][offset:P, cols],
                         start=(g == 0),
@@ -278,7 +309,15 @@ def tile_ffnn_encoder_pc_kernel(
         def layer_norm(m, accs):
             r = norm.tile([P, D], F32, name="r")
             r_sums = norm.tile([P, D_HALVES], F32, name="r_sums")
-            for half in range(D_HALVES):
+            neg_mean = norm.tile([P, 1], F32, name="neg_mean")
+            squares = norm.tile([P, D], BF16, name="squares")
+            sum_sq = norm.tile([P, 1], F32, name="sum_sq")
+            std = norm.tile([P, 1], F32, name="std")
+            scaled = norm.tile([P, D], F32, name="scaled")
+            rstd = norm.tile([P, 1], F32, name="rstd")
+            result = norm.tile([P, D], F32, name="result")
+
+            def add_residual(half):
                 cols = slice(half * N_TILE, (half + 1) * N_TILE)
                 nc.vector.scalar_tensor_tensor(
                     out=r[:, cols],
@@ -289,32 +328,41 @@ def tile_ffnn_encoder_pc_kernel(
                     op1=ADD,
                     accum_out=r_sums[:, half : half + 1],
                 )
-            neg_mean = norm.tile([P, 1], F32, name="neg_mean")
-            nc.vector.tensor_scalar(
-                out=neg_mean[:],
-                in0=r_sums[:, 0:1],
-                scalar1=r_sums[:, 1:2],
-                scalar2=-1.0 / D,
-                op0=ADD,
-                op1=MULT,
-            )
-            squares = norm.tile([P, D], BF16, name="squares")
-            sum_sq = norm.tile([P, 1], F32, name="sum_sq")
-            nc.scalar.activation(
-                out=squares[:], in_=r[:], func=ACT.Square, bias=neg_mean[:, 0:1], accum_out=sum_sq[:]
-            )
-            std = norm.tile([P, 1], F32, name="std")
-            nc.scalar.activation(
-                out=std[:], in_=sum_sq[:], func=ACT.Sqrt, bias=eps[:, 0:1], scale=1.0 / D
-            )
-            scaled = norm.tile([P, D], F32, name="scaled")
-            nc.vector.scalar_tensor_tensor(
-                out=scaled[:], in0=r[:], scalar=neg_mean[:, 0:1], in1=g2_bc[:], op0=ADD, op1=MULT
-            )
-            rstd = norm.tile([P, 1], F32, name="rstd")
-            nc.vector.reciprocal(rstd[:], std[:])
-            result = norm.tile([P, D], F32, name="result")
-            for half in range(D_HALVES):
+
+            def statistics():
+                nc.vector.tensor_scalar(
+                    out=neg_mean[:],
+                    in0=r_sums[:, 0:1],
+                    scalar1=r_sums[:, 1:2],
+                    scalar2=-1.0 / D,
+                    op0=ADD,
+                    op1=MULT,
+                )
+                nc.scalar.activation(
+                    out=squares[:],
+                    in_=r[:],
+                    func=ACT.Square,
+                    bias=neg_mean[:, 0:1],
+                    accum_out=sum_sq[:],
+                )
+                nc.scalar.activation(
+                    out=std[:], in_=sum_sq[:], func=ACT.Sqrt, bias=eps[:, 0:1], scale=1.0 / D
+                )
+
+            def scale():
+                nc.vector.scalar_tensor_tensor(
+                    out=scaled[:],
+                    in0=r[:],
+                    scalar=neg_mean[:, 0:1],
+                    in1=g2_bc[:],
+                    op0=ADD,
+                    op1=MULT,
+                )
+
+            def invert():
+                nc.vector.reciprocal(rstd[:], std[:])
+
+            def finish(half):
                 cols = slice(half * N_TILE, (half + 1) * N_TILE)
                 nc.vector.scalar_tensor_tensor(
                     out=result[:, cols],
@@ -326,44 +374,74 @@ def tile_ffnn_encoder_pc_kernel(
                 )
                 nc.sync.dma_start(out=out_rows[m * P : (m + 1) * P, cols], in_=result[:, cols])
 
+            return add_residual, statistics, scale, invert, finish
+
+        permute_planes(0, 0)
+        permute_planes(1, 0)
+        for m in range(TOK_TILES):
+            transpose_h(m)
+            if m == 1:
+                permute_planes(0, 1)
+                quantise_h(0)
+        quantise_h(1)
+        permute_words(0)
+        permute_planes(1, 1)
+        permute_words(1)
         b1_to_partitions()
         broadcast_b2(0)
         broadcast_b2(1)
-        for m in range(TOK_TILES):
-            transpose_h(m)
-            residual(m, 0)
-            residual(m, 1)
-            if m % 2 == 1:
-                quantise_h(m // 2)
-        permute_planes(0)
-        permute_words(0)
-        permute_planes(1)
-        permute_words(1)
+        for half in range(D_HALVES):
+            residual_by_tensor(0, half)
 
+        last = F_CHUNKS - 1
         accs = {0: open_out_banks(psum_o)}
         for g in range(F_CHUNKS):
-            first_matmul(g)
+            first_matmul(g, 1 if g < last else 2)
+            if g == 0:
+                for i in range(2, 8):
+                    residual_by_vector(i // 2, i % 2)
             if g >= 1:
-                interleave(g - 1)
+                interleave(g - 1, 0)
+                interleave(g - 1, 1)
             if g + 2 < F_CHUNKS:
-                if g + 2 < 4:
-                    permute_planes(g + 2)
                 permute_words(g + 2)
             if g >= 1:
-                quantise_hid(g - 1)
+                quantise_hid(g - 1, 0)
+                quantise_hid(g - 1, 1)
             if g >= 2:
                 second_matmul(0, accs[0], [g - 2])
 
-        last = F_CHUNKS - 1
         accs[1] = open_out_banks(psum_a)
-        second_matmul(1, accs[1], range(last))
-        interleave(last)
-        quantise_hid(last)
-        second_matmul(0, accs[0], [last - 1, last])
-        layer_norm(0, accs[0])
-        second_matmul(1, accs[1], [last])
-        layer_norm(1, accs[1])
+        second_matmul(0, accs[0], [last - 1])
+        second_matmul(1, accs[1], range(4))
+        interleave(last, 0)
+        quantise_hid(last, 0)
+        interleave(last, 1)
+        quantise_hid(last, 1)
+        second_matmul(0, accs[0], [last])
+        second_matmul(1, accs[1], range(4, F_CHUNKS))
         for m in range(2, TOK_TILES):
             accs[m] = open_out_banks(psum_a)
-            second_matmul(m, accs[m], range(F_CHUNKS))
-            layer_norm(m, accs[m])
+            if m < TOK_TILES - 1:
+                second_matmul(m, accs[m], range(F_CHUNKS))
+            else:
+                second_matmul(m, accs[m], range(F_CHUNKS), [0])
+                second_matmul(m, accs[m], range(F_CHUNKS), [1])
+
+        before = None
+        for m in range(TOK_TILES):
+            add_residual, statistics, scale, invert, finish = layer_norm(m, accs[m])
+            add_residual(0)
+            if before:
+                before[0]()
+            add_residual(1)
+            if before:
+                before[1](0)
+            statistics()
+            if before:
+                before[1](1)
+            scale()
+            before = (invert, finish)
+        before[0]()
+        before[1](0)
+        before[1](1)

@@ -234,8 +234,8 @@ def tile_ffnn_encoder_pc_kernel(
 
         def permute_words(g):
             nc.vector.tensor_copy(
-                out=w1_words[g][:].bitcast(I32).rearrange("p c (t m) -> p c t m", t=PACK),
-                in_=w1_raw[g][:].bitcast(I32).rearrange("p c (m t) -> p c t m", t=PACK),
+                out=w1_words[g][:].bitcast(I32).rearrange("p c (t m) -> p c m t", t=PACK),
+                in_=w1_raw[g][:].bitcast(I32).rearrange("p c (m t) -> p c m t", t=PACK),
             )
 
         hid_tiles = {}

@@ -25,6 +25,7 @@ D_PASSES = D // K_PASS
 F_CHUNKS = F // K_PASS
 D_HALVES = D // N_TILE
 PLANES_PER_TILE = 4
+RESIDUALS_BY_TENSOR = 2
 PACK = 4
 HALF = TOKENS // 2
 
@@ -98,7 +99,7 @@ def tile_ffnn_encoder_pc_kernel(
         eps = keep.tile([P, 1], F32, name="eps")
         first_sqrt = keep.tile([P, 1], F32, name="first_sqrt")
 
-        nc.gpsimd.memset(bias_rows[:], 0.0)
+        nc.vector.memset(bias_rows[:], 0.0)
         nc.vector.memset(eps[:], EPS)
         nc.vector.memset(w1_raw_planes[:].rearrange("p c n -> p (c n)").bitcast(I32), 0)
         for plane_tile in w2_planes:
@@ -139,16 +140,20 @@ def tile_ffnn_encoder_pc_kernel(
                     in_=scales[:, 4 * quadrant : 4 * quadrant + 4, :].bitcast(I32),
                 )
 
-        load_w1_planes(0, range(4))
-        for m in range(TOK_TILES):
-            load_h(m)
-        load_w1_planes(1, range(4))
-        load_w1_chunk(0)
-        nc.sync.dma_start(out=bias_rows[0:F_CHUNKS, :], in_=b1.rearrange("(r c) -> r c", c=N_TILE))
-        nc.sync.dma_start(
+        nc.scalar.dma_start(
+            out=bias_rows[0:F_CHUNKS, :], in_=b1.rearrange("(r c) -> r c", c=N_TILE)
+        )
+        nc.scalar.dma_start(
             out=bias_rows[F_CHUNKS : F_CHUNKS + D_HALVES, :],
             in_=b2.rearrange("(r c) -> r c", c=N_TILE),
         )
+        load_w1_planes(0, range(4))
+        load_h(0)
+        load_h(1)
+        load_w1_planes(1, range(4))
+        load_w1_chunk(0)
+        load_h(2)
+        load_h(3)
         for g in range(1, 4):
             load_w1_chunk(g)
         load_w2_planes(0)
@@ -241,30 +246,31 @@ def tile_ffnn_encoder_pc_kernel(
         hid_tiles = {}
         grouped_tiles = {}
 
-        def first_matmul(g, pieces=1):
-            hid = stream.tile([P, PACK, TOKENS], BF16, name="hid")
-            hid_tiles[g] = hid
+        def first_matmul(g, first, width):
+            if first == 0:
+                hid_tiles[g] = stream.tile([P, PACK, TOKENS], BF16, name="hid")
+            tokens = slice(first, first + width)
             x, q = divmod(g, 2)
-            width = TOKENS // pieces
-            for i in range(pieces):
-                tokens = slice(width * i, width * (i + 1))
-                for t in range(PACK):
-                    acc = psum_a.tile([P, width], F32, tag="bank", name="hid_acc")
-                    for c in range(D_PASSES):
-                        nc.tensor.matmul_mx(
-                            out=acc[:],
-                            lhsT=w1_words[g][:, c, t * P : (t + 1) * P].bitcast(FP8X4),
-                            lhsT_scale=w1_planes[q][
-                                4 * x : P, c * K_PASS + t * P : c * K_PASS + (t + 1) * P
-                            ],
-                            rhs=hq_words[c][:, tokens].bitcast(FP8X4),
-                            rhs_scale=hq_scales[c][:, tokens],
-                            start=(c == 0),
-                            stop=(c == D_PASSES - 1),
-                        )
-                    nc.scalar.activation(
-                        out=hid[:, t, tokens], in_=acc[:], func=ACT.Relu, bias=b1_cols[:, t, g : g + 1]
+            for t in range(PACK):
+                acc = psum_a.tile([P, width], F32, tag="bank", name="hid_acc")
+                for c in range(D_PASSES):
+                    nc.tensor.matmul_mx(
+                        out=acc[:],
+                        lhsT=w1_words[g][:, c, t * P : (t + 1) * P].bitcast(FP8X4),
+                        lhsT_scale=w1_planes[q][
+                            4 * x : P, c * K_PASS + t * P : c * K_PASS + (t + 1) * P
+                        ],
+                        rhs=hq_words[c][:, tokens].bitcast(FP8X4),
+                        rhs_scale=hq_scales[c][:, tokens],
+                        start=(c == 0),
+                        stop=(c == D_PASSES - 1),
                     )
+                nc.scalar.activation(
+                    out=hid_tiles[g][:, t, tokens],
+                    in_=acc[:],
+                    func=ACT.Relu,
+                    bias=b1_cols[:, t, g : g + 1],
+                )
 
         def interleave(g, half):
             if half == 0:
@@ -273,7 +279,8 @@ def tile_ffnn_encoder_pc_kernel(
                 )
             cols = slice(HALF * half, HALF * (half + 1))
             nc.vector.tensor_copy(
-                out=grouped_tiles[g][:, cols, :], in_=hid_tiles[g][:, :, cols].rearrange("p t n -> p n t")
+                out=grouped_tiles[g][:, cols, :].rearrange("p (n i) t -> p n t i", i=4),
+                in_=hid_tiles[g][:, :, cols].rearrange("p t (n i) -> p n t i", i=4),
             )
 
         def quantise_hid(g, half):
@@ -378,32 +385,41 @@ def tile_ffnn_encoder_pc_kernel(
 
         permute_planes(0, 0)
         permute_planes(1, 0)
-        for m in range(TOK_TILES):
-            transpose_h(m)
-            if m == 1:
-                permute_planes(0, 1)
-                quantise_h(0)
-        quantise_h(1)
-        permute_words(0)
-        permute_planes(1, 1)
-        permute_words(1)
         b1_to_partitions()
         broadcast_b2(0)
         broadcast_b2(1)
-        for half in range(D_HALVES):
-            residual_by_tensor(0, half)
+        transpose_h(0)
+        transpose_h(1)
+        permute_planes(0, 1)
+        quantise_h(0)
+        for i in range(RESIDUALS_BY_TENSOR):
+            residual_by_tensor(i // 2, i % 2)
+        permute_words(0)
+        transpose_h(2)
+        transpose_h(3)
+        first_matmul(0, 0, HALF)
+        quantise_h(1)
+        permute_planes(1, 1)
+        permute_words(1)
 
         last = F_CHUNKS - 1
         accs = {0: open_out_banks(psum_o)}
         for g in range(F_CHUNKS):
-            first_matmul(g, 1 if g < last else 2)
             if g == 0:
-                for i in range(2, 8):
-                    residual_by_vector(i // 2, i % 2)
+                first_matmul(0, HALF, HALF)
+                permute_words(2)
+                residual_by_vector(1, 0)
+                residual_by_vector(1, 1)
+                residual_by_vector(2, 0)
+            elif g < last:
+                first_matmul(g, 0, TOKENS)
+            else:
+                first_matmul(g, 0, HALF)
+                first_matmul(g, HALF, HALF)
             if g >= 1:
                 interleave(g - 1, 0)
                 interleave(g - 1, 1)
-            if g + 2 < F_CHUNKS:
+            if 0 < g < last - 1:
                 permute_words(g + 2)
             if g >= 1:
                 quantise_hid(g - 1, 0)
@@ -413,13 +429,13 @@ def tile_ffnn_encoder_pc_kernel(
 
         accs[1] = open_out_banks(psum_a)
         second_matmul(0, accs[0], [last - 1])
-        second_matmul(1, accs[1], range(4))
+        second_matmul(1, accs[1], range(2))
         interleave(last, 0)
         quantise_hid(last, 0)
         interleave(last, 1)
         quantise_hid(last, 1)
         second_matmul(0, accs[0], [last])
-        second_matmul(1, accs[1], range(4, F_CHUNKS))
+        second_matmul(1, accs[1], range(2, F_CHUNKS))
         for m in range(2, TOK_TILES):
             accs[m] = open_out_banks(psum_a)
             if m < TOK_TILES - 1:
@@ -441,6 +457,11 @@ def tile_ffnn_encoder_pc_kernel(
             if before:
                 before[1](1)
             scale()
+            if m == 0:
+                residual_by_vector(2, 1)
+            elif m == 1:
+                residual_by_vector(3, 0)
+                residual_by_vector(3, 1)
             before = (invert, finish)
         before[0]()
         before[1](0)

@@ -25,7 +25,7 @@ D_PASSES = D // K_PASS
 F_CHUNKS = F // K_PASS
 D_HALVES = D // N_TILE
 PLANES_PER_TILE = 4
-RESIDUALS_BY_TENSOR = 2
+RESIDUALS_BY_TENSOR = 4
 PACK = 4
 HALF = TOKENS // 2
 
@@ -97,7 +97,7 @@ def tile_ffnn_encoder_pc_kernel(
         ident_f32 = keep.tile([P, P], F32, name="ident_f32")
         ident_bf16 = keep.tile([P, P], BF16, name="ident_bf16")
         eps = keep.tile([P, 1], F32, name="eps")
-        first_sqrt = keep.tile([P, 1], F32, name="first_sqrt")
+        first_rsqrt = keep.tile([P, 1], F32, name="first_rsqrt")
 
         nc.vector.memset(bias_rows[:], 0.0)
         nc.vector.memset(eps[:], EPS)
@@ -106,7 +106,7 @@ def tile_ffnn_encoder_pc_kernel(
             nc.vector.memset(plane_tile[:].bitcast(I32), 0)
         make_identity(nc, ident_bf16[:])
         make_identity(nc, ident_f32[:])
-        nc.scalar.activation(out=first_sqrt[:], in_=eps[:], func=ACT.Sqrt)
+        nc.scalar.activation(out=first_rsqrt[:], in_=eps[:], func=ACT.Abs_reciprocal_sqrt)
 
         def load_h(m):
             nc.sync.dma_start(out=x_sb[m][:], in_=h_rows[m * P : (m + 1) * P, :])
@@ -291,20 +291,24 @@ def tile_ffnn_encoder_pc_kernel(
                 in_=grouped_tiles[g][:, cols, :].rearrange("p n t -> p (n t)"),
             )
 
-        def open_out_banks(pool):
+        half_row = slice(0, N_TILE), slice(N_TILE, D)
+        pieces = [half_row] * (TOK_TILES - 1)
+        pieces.append((slice(0, N_TILE), slice(N_TILE, 3 * N_TILE // 2), slice(3 * N_TILE // 2, D)))
+
+        def open_out_banks(pool, m):
             return [
-                pool.tile([P, N_TILE], F32, tag="bank", name="out_acc%d" % half)
-                for half in range(D_HALVES)
+                pool.tile([P, cols.stop - cols.start], F32, tag="bank", name="out_acc")
+                for cols in pieces[m]
             ]
 
-        def second_matmul(m, accs, chunks, halves=(0, 1)):
+        def second_matmul(m, accs, chunks, which=(0, 1)):
             rows = slice(m * P, (m + 1) * P)
             for g in chunks:
-                for half in halves:
+                for i in which:
                     offset = 4 * (g % PLANES_PER_TILE)
-                    cols = slice(half * N_TILE, (half + 1) * N_TILE)
+                    cols = pieces[m][i]
                     nc.tensor.matmul_mx(
-                        out=accs[half][:],
+                        out=accs[i][:],
                         lhsT=hidq_words[g][:, rows].bitcast(FP8X4),
                         lhsT_scale=hidq_scales[g][:, rows],
                         rhs=w2_words[g][:, cols].bitcast(FP8X4),
@@ -315,32 +319,40 @@ def tile_ffnn_encoder_pc_kernel(
 
         def layer_norm(m, accs):
             r = norm.tile([P, D], F32, name="r")
-            r_sums = norm.tile([P, D_HALVES], F32, name="r_sums")
+            r_sums = norm.tile([P, 3], F32, name="r_sums")
+            two_sums = norm.tile([P, 1], F32, name="two_sums")
             neg_mean = norm.tile([P, 1], F32, name="neg_mean")
             squares = norm.tile([P, D], BF16, name="squares")
             sum_sq = norm.tile([P, 1], F32, name="sum_sq")
-            std = norm.tile([P, 1], F32, name="std")
             scaled = norm.tile([P, D], F32, name="scaled")
             rstd = norm.tile([P, 1], F32, name="rstd")
             result = norm.tile([P, D], F32, name="result")
 
-            def add_residual(half):
-                cols = slice(half * N_TILE, (half + 1) * N_TILE)
+            def add_residual(i):
+                cols = pieces[m][i]
                 nc.vector.scalar_tensor_tensor(
                     out=r[:, cols],
-                    in0=accs[half][:],
+                    in0=accs[i][:],
                     scalar=1.0,
                     in1=res[m][:, cols],
                     op0=MULT,
                     op1=ADD,
-                    accum_out=r_sums[:, half : half + 1],
+                    accum_out=r_sums[:, i : i + 1],
+                )
+
+            def add_two_sums():
+                nc.vector.tensor_scalar(
+                    out=two_sums[:], in0=r_sums[:, 0:1], scalar1=r_sums[:, 1:2], scalar2=None, op0=ADD
                 )
 
             def statistics():
+                first, second = r_sums[:, 0:1], r_sums[:, 1:2]
+                if len(pieces[m]) == 3:
+                    first, second = two_sums[:], r_sums[:, 2:3]
                 nc.vector.tensor_scalar(
                     out=neg_mean[:],
-                    in0=r_sums[:, 0:1],
-                    scalar1=r_sums[:, 1:2],
+                    in0=first,
+                    scalar1=second,
                     scalar2=-1.0 / D,
                     op0=ADD,
                     op1=MULT,
@@ -353,7 +365,11 @@ def tile_ffnn_encoder_pc_kernel(
                     accum_out=sum_sq[:],
                 )
                 nc.scalar.activation(
-                    out=std[:], in_=sum_sq[:], func=ACT.Sqrt, bias=eps[:, 0:1], scale=1.0 / D
+                    out=rstd[:],
+                    in_=sum_sq[:],
+                    func=ACT.Abs_reciprocal_sqrt,
+                    bias=eps[:, 0:1],
+                    scale=1.0 / D,
                 )
 
             def scale():
@@ -365,9 +381,6 @@ def tile_ffnn_encoder_pc_kernel(
                     op0=ADD,
                     op1=MULT,
                 )
-
-            def invert():
-                nc.vector.reciprocal(rstd[:], std[:])
 
             def finish(half):
                 cols = slice(half * N_TILE, (half + 1) * N_TILE)
@@ -381,7 +394,7 @@ def tile_ffnn_encoder_pc_kernel(
                 )
                 nc.sync.dma_start(out=out_rows[m * P : (m + 1) * P, cols], in_=result[:, cols])
 
-            return add_residual, statistics, scale, invert, finish
+            return add_residual, add_two_sums, statistics, scale, finish
 
         permute_planes(0, 0)
         permute_planes(1, 0)
@@ -403,14 +416,11 @@ def tile_ffnn_encoder_pc_kernel(
         permute_words(1)
 
         last = F_CHUNKS - 1
-        accs = {0: open_out_banks(psum_o)}
+        accs = {0: open_out_banks(psum_o, 0)}
         for g in range(F_CHUNKS):
             if g == 0:
                 first_matmul(0, HALF, HALF)
                 permute_words(2)
-                residual_by_vector(1, 0)
-                residual_by_vector(1, 1)
-                residual_by_vector(2, 0)
             elif g < last:
                 first_matmul(g, 0, TOKENS)
             else:
@@ -421,48 +431,42 @@ def tile_ffnn_encoder_pc_kernel(
                 interleave(g - 1, 1)
             if 0 < g < last - 1:
                 permute_words(g + 2)
+            i = RESIDUALS_BY_TENSOR + g
+            if i < 2 * TOK_TILES:
+                residual_by_vector(i // 2, i % 2)
             if g >= 1:
                 quantise_hid(g - 1, 0)
                 quantise_hid(g - 1, 1)
             if g >= 2:
                 second_matmul(0, accs[0], [g - 2])
 
-        accs[1] = open_out_banks(psum_a)
+        accs[1] = open_out_banks(psum_a, 1)
         second_matmul(0, accs[0], [last - 1])
-        second_matmul(1, accs[1], range(2))
+        second_matmul(1, accs[1], range(1))
         interleave(last, 0)
         quantise_hid(last, 0)
         interleave(last, 1)
         quantise_hid(last, 1)
         second_matmul(0, accs[0], [last])
-        second_matmul(1, accs[1], range(2, F_CHUNKS))
+        second_matmul(1, accs[1], range(1, F_CHUNKS))
         for m in range(2, TOK_TILES):
-            accs[m] = open_out_banks(psum_a)
-            if m < TOK_TILES - 1:
-                second_matmul(m, accs[m], range(F_CHUNKS))
-            else:
-                second_matmul(m, accs[m], range(F_CHUNKS), [0])
-                second_matmul(m, accs[m], range(F_CHUNKS), [1])
+            accs[m] = open_out_banks(psum_a, m)
+            for i in range(len(pieces[m])):
+                second_matmul(m, accs[m], range(F_CHUNKS), [i])
 
         before = None
         for m in range(TOK_TILES):
-            add_residual, statistics, scale, invert, finish = layer_norm(m, accs[m])
+            add_residual, add_two_sums, statistics, scale, finish = layer_norm(m, accs[m])
             add_residual(0)
             if before:
-                before[0]()
+                before(0)
+                before(1)
             add_residual(1)
-            if before:
-                before[1](0)
+            if len(pieces[m]) == 3:
+                add_two_sums()
+                add_residual(2)
             statistics()
-            if before:
-                before[1](1)
             scale()
-            if m == 0:
-                residual_by_vector(2, 1)
-            elif m == 1:
-                residual_by_vector(3, 0)
-                residual_by_vector(3, 1)
-            before = (invert, finish)
-        before[0]()
-        before[1](0)
-        before[1](1)
+            before = finish
+        before(0)
+        before(1)

@@ -25,7 +25,7 @@ D_PASSES = D // K_PASS
 F_CHUNKS = F // K_PASS
 D_HALVES = D // N_TILE
 PLANES_PER_TILE = 4
-RESIDUALS_BY_TENSOR = 4
+RESIDUALS_BY_TENSOR = 2
 PACK = 4
 HALF = TOKENS // 2
 
@@ -47,7 +47,7 @@ def tile_ffnn_encoder_pc_kernel(
         psum_a = ctx.enter_context(tc.psum_pool(name="psum_a", bufs=6))
         psum_o = ctx.enter_context(tc.psum_pool(name="psum_o", bufs=2))
 
-        x_sb = [keep.tile([P, D], BF16, name="x_sb%d" % m) for m in range(TOK_TILES)]
+        x_pairs = [keep.tile([P, 2, D], BF16, name="x_pair%d" % i) for i in range(2)]
         w1_raw = [
             keep.tile([P, D_PASSES, N_TILE], U32, name="w1_raw%d" % g, align_bytes=64)
             for g in range(F_CHUNKS)
@@ -69,8 +69,8 @@ def tile_ffnn_encoder_pc_kernel(
             for j in range(F_CHUNKS // PLANES_PER_TILE)
         ]
         h_grouped = [
-            keep.tile([P, D_PASSES, HALF, PACK], BF16, name="h_grouped%d" % i, align_bytes=64)
-            for i in range(2)
+            keep.tile([P, TOKENS, PACK], BF16, name="h_grouped%d" % c, align_bytes=64)
+            for c in range(D_PASSES)
         ]
         hq_words = [
             keep.tile([P, TOKENS], U32, name="hq_words%d" % c, align_bytes=64)
@@ -108,8 +108,20 @@ def tile_ffnn_encoder_pc_kernel(
         make_identity(nc, ident_f32[:])
         nc.scalar.activation(out=first_rsqrt[:], in_=eps[:], func=ACT.Abs_reciprocal_sqrt)
 
-        def load_h(m):
-            nc.sync.dma_start(out=x_sb[m][:], in_=h_rows[m * P : (m + 1) * P, :])
+        def load_h(i, c):
+            rows = h_rows[HALF * i : HALF * (i + 1), K_PASS * c : K_PASS * (c + 1)]
+            nc.sync.dma_start(
+                out=x_pairs[i][:, :, K_PASS * c : K_PASS * (c + 1)],
+                in_=rows.rearrange("(e p) k -> p e k", e=2),
+            )
+
+        def load_w1_pass(g, c):
+            nc.sync.dma_start(
+                out=w1_raw[g][:, c, :].bitcast(I32),
+                in_=W1_words[c, :, N_TILE * g : N_TILE * (g + 1), :]
+                .rearrange("p n t -> p (n t)")
+                .bitcast(I32),
+            )
 
         def load_w1_chunk(g):
             by_partition = W1_words.rearrange("c p n t -> p c (n t)")
@@ -147,13 +159,11 @@ def tile_ffnn_encoder_pc_kernel(
             out=bias_rows[F_CHUNKS : F_CHUNKS + D_HALVES, :],
             in_=b2.rearrange("(r c) -> r c", c=N_TILE),
         )
-        load_w1_planes(0, range(4))
-        load_h(0)
-        load_h(1)
-        load_w1_planes(1, range(4))
-        load_w1_chunk(0)
-        load_h(2)
-        load_h(3)
+        for c in range(D_PASSES):
+            load_w1_planes(c, range(4))
+            load_h(0, c)
+            load_h(1, c)
+            load_w1_pass(0, c)
         for g in range(1, 4):
             load_w1_chunk(g)
         load_w2_planes(0)
@@ -191,7 +201,7 @@ def tile_ffnn_encoder_pc_kernel(
             cols = slice(half * N_TILE, (half + 1) * N_TILE)
             bank = psum_o.tile([P, N_TILE], F32, tag="bank", name="res_bank")
             nc.tensor.matmul(
-                out=bank[:], lhsT=ident_bf16[:], rhs=x_sb[m][:, cols], start=True, stop=False
+                out=bank[:], lhsT=ident_bf16[:], rhs=x_pairs[m // 2][:, m % 2, cols], start=True, stop=False
             )
             spread_b2(bank, half, False, True)
             nc.scalar.copy(out=res[m][:, cols], in_=bank[:])
@@ -199,33 +209,32 @@ def tile_ffnn_encoder_pc_kernel(
         def residual_by_vector(m, half):
             cols = slice(half * N_TILE, (half + 1) * N_TILE)
             nc.vector.tensor_tensor(
-                out=res[m][:, cols], in0=x_sb[m][:, cols], in1=b2_bc[:, cols], op=ADD
+                out=res[m][:, cols], in0=x_pairs[m // 2][:, m % 2, cols], in1=b2_bc[:, cols], op=ADD
             )
 
-        def transpose_h(m):
-            x_as_words = x_sb[m][:].bitcast(F32)
-            bank = psum_a.tile([P, D_PASSES, 2, P], F32, tag="bank", name="hT_bank")
-            for c in range(D_PASSES):
+        def transpose_h(i, c):
+            bank = psum_a.tile([P, 2, 2, P], F32, tag="bank", name="hT_bank")
+            for e in range(2):
+                x_as_words = x_pairs[i][:, e, :].bitcast(F32)
                 for u in range(2):
                     nc.tensor.transpose(
-                        bank[:, c, u, :],
+                        bank[:, e, u, :],
                         x_as_words[:, 256 * c + u : 256 * (c + 1) : 2],
                         ident_f32[:],
                     )
-            tokens = slice((m % 2) * P, (m % 2 + 1) * P)
-            words = h_grouped[m // 2][:].rearrange("p c n k -> p (c n k)").bitcast(F32)
-            words = words.rearrange("p (c n u) -> p c n u", c=D_PASSES, u=2)
-            copy = nc.vector.tensor_copy if m % 2 == 0 else nc.scalar.copy
-            copy(out=words[:, :, tokens, :], in_=bank[:].rearrange("p c u n -> p c n u"))
+            words = h_grouped[c][:, HALF * i : HALF * (i + 1), :].rearrange("p n k -> p (n k)")
+            copy = nc.vector.tensor_copy if i == 0 else nc.scalar.copy
+            copy(
+                out=words.bitcast(F32).rearrange("p (e n u) -> p e n u", e=2, u=2),
+                in_=bank[:].rearrange("p e u n -> p e n u"),
+            )
 
-        def quantise_h(i):
-            cols = slice(HALF * i, HALF * (i + 1))
-            for c in range(D_PASSES):
-                nc.vector.quantize_mx(
-                    out=hq_words[c][:, cols].bitcast(FP8X4),
-                    scales=hq_scales[c][:, cols],
-                    in_=h_grouped[i][:, c, :, :].rearrange("p n k -> p (n k)"),
-                )
+        def quantise_h(c):
+            nc.vector.quantize_mx(
+                out=hq_words[c][:].bitcast(FP8X4),
+                scales=hq_scales[c][:],
+                in_=h_grouped[c][:].rearrange("p n k -> p (n k)"),
+            )
 
         def permute_planes(q, c):
             nc.vector.tensor_copy(
@@ -237,40 +246,46 @@ def tile_ffnn_encoder_pc_kernel(
                 ),
             )
 
-        def permute_words(g):
+        def permute_words(g, first=0, passes=D_PASSES):
+            c = slice(first, first + passes)
             nc.vector.tensor_copy(
-                out=w1_words[g][:].bitcast(I32).rearrange("p c (t m) -> p c m t", t=PACK),
-                in_=w1_raw[g][:].bitcast(I32).rearrange("p c (m t) -> p c m t", t=PACK),
+                out=w1_words[g][:, c, :].bitcast(I32).rearrange("p c (t m) -> p c m t", t=PACK),
+                in_=w1_raw[g][:, c, :].bitcast(I32).rearrange("p c (m t) -> p c m t", t=PACK),
             )
 
         hid_tiles = {}
         grouped_tiles = {}
 
-        def first_matmul(g, first, width):
+        def first_matmul(g, first=0, width=TOKENS, by_pass=False):
             if first == 0:
                 hid_tiles[g] = stream.tile([P, PACK, TOKENS], BF16, name="hid")
             tokens = slice(first, first + width)
             x, q = divmod(g, 2)
-            for t in range(PACK):
-                acc = psum_a.tile([P, width], F32, tag="bank", name="hid_acc")
-                for c in range(D_PASSES):
-                    nc.tensor.matmul_mx(
-                        out=acc[:],
-                        lhsT=w1_words[g][:, c, t * P : (t + 1) * P].bitcast(FP8X4),
-                        lhsT_scale=w1_planes[q][
-                            4 * x : P, c * K_PASS + t * P : c * K_PASS + (t + 1) * P
-                        ],
-                        rhs=hq_words[c][:, tokens].bitcast(FP8X4),
-                        rhs_scale=hq_scales[c][:, tokens],
-                        start=(c == 0),
-                        stop=(c == D_PASSES - 1),
-                    )
-                nc.scalar.activation(
-                    out=hid_tiles[g][:, t, tokens],
-                    in_=acc[:],
-                    func=ACT.Relu,
-                    bias=b1_cols[:, t, g : g + 1],
+            banks = [
+                psum_a.tile([P, width], F32, tag="bank", name="hid_acc%d" % t) for t in range(PACK)
+            ]
+            order = [(t, c) for t in range(PACK) for c in range(D_PASSES)]
+            if by_pass:
+                order = [(t, c) for c in range(D_PASSES) for t in range(PACK)]
+            for t, c in order:
+                nc.tensor.matmul_mx(
+                    out=banks[t][:],
+                    lhsT=w1_words[g][:, c, t * P : (t + 1) * P].bitcast(FP8X4),
+                    lhsT_scale=w1_planes[q][
+                        4 * x : P, c * K_PASS + t * P : c * K_PASS + (t + 1) * P
+                    ],
+                    rhs=hq_words[c][:, tokens].bitcast(FP8X4),
+                    rhs_scale=hq_scales[c][:, tokens],
+                    start=(c == 0),
+                    stop=(c == D_PASSES - 1),
                 )
+                if c == D_PASSES - 1:
+                    nc.scalar.activation(
+                        out=hid_tiles[g][:, t, tokens],
+                        in_=banks[t][:],
+                        func=ACT.Relu,
+                        bias=b1_cols[:, t, g : g + 1],
+                    )
 
         def interleave(g, half):
             if half == 0:
@@ -401,28 +416,30 @@ def tile_ffnn_encoder_pc_kernel(
         b1_to_partitions()
         broadcast_b2(0)
         broadcast_b2(1)
-        transpose_h(0)
-        transpose_h(1)
-        permute_planes(0, 1)
+        transpose_h(0, 0)
+        transpose_h(1, 0)
+        permute_words(0, 0, 1)
         quantise_h(0)
-        for i in range(RESIDUALS_BY_TENSOR):
-            residual_by_tensor(i // 2, i % 2)
-        permute_words(0)
-        transpose_h(2)
-        transpose_h(3)
-        first_matmul(0, 0, HALF)
+        for m in range(RESIDUALS_BY_TENSOR):
+            residual_by_tensor(m, 0)
+        permute_planes(0, 1)
+        transpose_h(0, 1)
+        transpose_h(1, 1)
+        permute_words(0, 1, 1)
         quantise_h(1)
+        first_matmul(0, by_pass=True)
         permute_planes(1, 1)
         permute_words(1)
 
         last = F_CHUNKS - 1
+        by_vector = [(m, 1) for m in range(RESIDUALS_BY_TENSOR)]
+        by_vector += [(m, half) for m in range(RESIDUALS_BY_TENSOR, TOK_TILES) for half in range(2)]
         accs = {0: open_out_banks(psum_o, 0)}
         for g in range(F_CHUNKS):
             if g == 0:
-                first_matmul(0, HALF, HALF)
                 permute_words(2)
             elif g < last:
-                first_matmul(g, 0, TOKENS)
+                first_matmul(g)
             else:
                 first_matmul(g, 0, HALF)
                 first_matmul(g, HALF, HALF)
@@ -431,9 +448,8 @@ def tile_ffnn_encoder_pc_kernel(
                 interleave(g - 1, 1)
             if 0 < g < last - 1:
                 permute_words(g + 2)
-            i = RESIDUALS_BY_TENSOR + g
-            if i < 2 * TOK_TILES:
-                residual_by_vector(i // 2, i % 2)
+            if g < len(by_vector):
+                residual_by_vector(*by_vector[g])
             if g >= 1:
                 quantise_hid(g - 1, 0)
                 quantise_hid(g - 1, 1)
@@ -449,24 +465,24 @@ def tile_ffnn_encoder_pc_kernel(
         quantise_hid(last, 1)
         second_matmul(0, accs[0], [last])
         second_matmul(1, accs[1], range(1, F_CHUNKS))
-        for m in range(2, TOK_TILES):
-            accs[m] = open_out_banks(psum_a, m)
-            for i in range(len(pieces[m])):
-                second_matmul(m, accs[m], range(F_CHUNKS), [i])
 
-        before = None
         for m in range(TOK_TILES):
+            if 2 <= m + 1 < TOK_TILES:
+                accs[m + 1] = open_out_banks(psum_a, m + 1)
+                for i in range(len(pieces[m + 1])):
+                    second_matmul(m + 1, accs[m + 1], range(F_CHUNKS), [i])
             add_residual, add_two_sums, statistics, scale, finish = layer_norm(m, accs[m])
             add_residual(0)
-            if before:
-                before(0)
-                before(1)
+            if m >= 2:
+                finish_before(0)
+                finish_before(1)
             add_residual(1)
             if len(pieces[m]) == 3:
                 add_two_sums()
                 add_residual(2)
             statistics()
             scale()
-            before = finish
-        before(0)
-        before(1)
+            if m in (0, TOK_TILES - 1):
+                finish(0)
+                finish(1)
+            finish_before = finish

@@ -69,8 +69,8 @@ def tile_ffnn_encoder_pc_kernel(
             for j in range(F_CHUNKS // PLANES_PER_TILE)
         ]
         h_grouped = [
-            keep.tile([P, TOKENS, PACK], BF16, name="h_grouped%d" % c, align_bytes=64)
-            for c in range(D_PASSES)
+            keep.tile([P, D_PASSES, HALF, PACK], BF16, name="h_grouped%d" % i, align_bytes=64)
+            for i in range(2)
         ]
         hq_words = [
             keep.tile([P, TOKENS], U32, name="hq_words%d" % c, align_bytes=64)
@@ -108,19 +108,10 @@ def tile_ffnn_encoder_pc_kernel(
         make_identity(nc, ident_f32[:])
         nc.scalar.activation(out=first_rsqrt[:], in_=eps[:], func=ACT.Abs_reciprocal_sqrt)
 
-        def load_h(i, c):
-            rows = h_rows[HALF * i : HALF * (i + 1), K_PASS * c : K_PASS * (c + 1)]
+        def load_h(i):
             nc.sync.dma_start(
-                out=x_pairs[i][:, :, K_PASS * c : K_PASS * (c + 1)],
-                in_=rows.rearrange("(e p) k -> p e k", e=2),
-            )
-
-        def load_w1_pass(g, c):
-            nc.sync.dma_start(
-                out=w1_raw[g][:, c, :].bitcast(I32),
-                in_=W1_words[c, :, N_TILE * g : N_TILE * (g + 1), :]
-                .rearrange("p n t -> p (n t)")
-                .bitcast(I32),
+                out=x_pairs[i][:],
+                in_=h_rows[HALF * i : HALF * (i + 1), :].rearrange("(e p) k -> p e k", e=2),
             )
 
         def load_w1_chunk(g):
@@ -136,8 +127,8 @@ def tile_ffnn_encoder_pc_kernel(
                 in_=W2_words[g].rearrange("p n t -> p (n t)").bitcast(I32),
             )
 
-        def load_w1_planes(c, quadrants):
-            for quadrant in quadrants:
+        def load_w1_planes(c):
+            for quadrant in range(4):
                 rows = W1_scales[c, 4 * quadrant : 4 * quadrant + 4, :]
                 nc.sync.dma_start(
                     out=w1_raw_planes[32 * quadrant : 32 * quadrant + 16, c, :].bitcast(I32),
@@ -152,22 +143,22 @@ def tile_ffnn_encoder_pc_kernel(
                     in_=scales[:, 4 * quadrant : 4 * quadrant + 4, :].bitcast(I32),
                 )
 
-        nc.scalar.dma_start(
+        load_h(0)
+        load_h(1)
+        load_w1_chunk(0)
+        nc.sync.dma_start(
             out=bias_rows[0:F_CHUNKS, :], in_=b1.rearrange("(r c) -> r c", c=N_TILE)
         )
-        nc.scalar.dma_start(
+        nc.sync.dma_start(
             out=bias_rows[F_CHUNKS : F_CHUNKS + D_HALVES, :],
             in_=b2.rearrange("(r c) -> r c", c=N_TILE),
         )
         for c in range(D_PASSES):
-            load_w1_planes(c, range(4))
-            load_h(0, c)
-            load_h(1, c)
-            load_w1_pass(0, c)
+            load_w1_planes(c)
         for g in range(1, 4):
             load_w1_chunk(g)
-        load_w2_planes(0)
-        load_w2_planes(1)
+        for j in range(F_CHUNKS // PLANES_PER_TILE):
+            load_w2_planes(j)
         for g in range(F_CHUNKS):
             load_w2_chunk(g)
             if g + 4 < F_CHUNKS:
@@ -212,29 +203,30 @@ def tile_ffnn_encoder_pc_kernel(
                 out=res[m][:, cols], in0=x_pairs[m // 2][:, m % 2, cols], in1=b2_bc[:, cols], op=ADD
             )
 
-        def transpose_h(i, c):
-            bank = psum_a.tile([P, 2, 2, P], F32, tag="bank", name="hT_bank")
-            for e in range(2):
-                x_as_words = x_pairs[i][:, e, :].bitcast(F32)
+        def transpose_h(m):
+            x_as_words = x_pairs[m // 2][:, m % 2, :].bitcast(F32)
+            bank = psum_a.tile([P, D_PASSES, 2, P], F32, tag="bank", name="hT_bank")
+            for c in range(D_PASSES):
                 for u in range(2):
                     nc.tensor.transpose(
-                        bank[:, e, u, :],
+                        bank[:, c, u, :],
                         x_as_words[:, 256 * c + u : 256 * (c + 1) : 2],
                         ident_f32[:],
                     )
-            words = h_grouped[c][:, HALF * i : HALF * (i + 1), :].rearrange("p n k -> p (n k)")
-            copy = nc.vector.tensor_copy if i == 0 else nc.scalar.copy
-            copy(
-                out=words.bitcast(F32).rearrange("p (e n u) -> p e n u", e=2, u=2),
-                in_=bank[:].rearrange("p e u n -> p e n u"),
-            )
+            tokens = slice((m % 2) * P, (m % 2 + 1) * P)
+            words = h_grouped[m // 2][:].rearrange("p c n k -> p (c n k)").bitcast(F32)
+            words = words.rearrange("p (c n u) -> p c n u", c=D_PASSES, u=2)
+            copy = nc.vector.tensor_copy if m % 2 == 0 else nc.scalar.copy
+            copy(out=words[:, :, tokens, :], in_=bank[:].rearrange("p c u n -> p c n u"))
 
-        def quantise_h(c):
-            nc.vector.quantize_mx(
-                out=hq_words[c][:].bitcast(FP8X4),
-                scales=hq_scales[c][:],
-                in_=h_grouped[c][:].rearrange("p n k -> p (n k)"),
-            )
+        def quantise_h(i):
+            cols = slice(HALF * i, HALF * (i + 1))
+            for c in range(D_PASSES):
+                nc.vector.quantize_mx(
+                    out=hq_words[c][:, cols].bitcast(FP8X4),
+                    scales=hq_scales[c][:, cols],
+                    in_=h_grouped[i][:, c, :, :].rearrange("p n k -> p (n k)"),
+                )
 
         def permute_planes(q, c):
             nc.vector.tensor_copy(
@@ -256,36 +248,31 @@ def tile_ffnn_encoder_pc_kernel(
         hid_tiles = {}
         grouped_tiles = {}
 
-        def first_matmul(g, first=0, width=TOKENS, by_pass=False):
+        def first_matmul(g, first=0, width=TOKENS):
             if first == 0:
                 hid_tiles[g] = stream.tile([P, PACK, TOKENS], BF16, name="hid")
             tokens = slice(first, first + width)
             x, q = divmod(g, 2)
-            banks = [
-                psum_a.tile([P, width], F32, tag="bank", name="hid_acc%d" % t) for t in range(PACK)
-            ]
-            order = [(t, c) for t in range(PACK) for c in range(D_PASSES)]
-            if by_pass:
-                order = [(t, c) for c in range(D_PASSES) for t in range(PACK)]
-            for t, c in order:
-                nc.tensor.matmul_mx(
-                    out=banks[t][:],
-                    lhsT=w1_words[g][:, c, t * P : (t + 1) * P].bitcast(FP8X4),
-                    lhsT_scale=w1_planes[q][
-                        4 * x : P, c * K_PASS + t * P : c * K_PASS + (t + 1) * P
-                    ],
-                    rhs=hq_words[c][:, tokens].bitcast(FP8X4),
-                    rhs_scale=hq_scales[c][:, tokens],
-                    start=(c == 0),
-                    stop=(c == D_PASSES - 1),
-                )
-                if c == D_PASSES - 1:
-                    nc.scalar.activation(
-                        out=hid_tiles[g][:, t, tokens],
-                        in_=banks[t][:],
-                        func=ACT.Relu,
-                        bias=b1_cols[:, t, g : g + 1],
+            for t in range(PACK):
+                acc = psum_a.tile([P, width], F32, tag="bank", name="hid_acc")
+                for c in range(D_PASSES):
+                    nc.tensor.matmul_mx(
+                        out=acc[:],
+                        lhsT=w1_words[g][:, c, t * P : (t + 1) * P].bitcast(FP8X4),
+                        lhsT_scale=w1_planes[q][
+                            4 * x : P, c * K_PASS + t * P : c * K_PASS + (t + 1) * P
+                        ],
+                        rhs=hq_words[c][:, tokens].bitcast(FP8X4),
+                        rhs_scale=hq_scales[c][:, tokens],
+                        start=(c == 0),
+                        stop=(c == D_PASSES - 1),
                     )
+                nc.scalar.activation(
+                    out=hid_tiles[g][:, t, tokens],
+                    in_=acc[:],
+                    func=ACT.Relu,
+                    bias=b1_cols[:, t, g : g + 1],
+                )
 
         def interleave(g, half):
             if half == 0:
@@ -411,23 +398,20 @@ def tile_ffnn_encoder_pc_kernel(
 
             return add_residual, add_two_sums, statistics, scale, finish
 
-        permute_planes(0, 0)
-        permute_planes(1, 0)
+        for m in range(TOK_TILES):
+            transpose_h(m)
+            if m % 2 == 1:
+                quantise_h(m // 2)
         b1_to_partitions()
         broadcast_b2(0)
         broadcast_b2(1)
-        transpose_h(0, 0)
-        transpose_h(1, 0)
-        permute_words(0, 0, 1)
-        quantise_h(0)
+        permute_words(0)
+        permute_planes(0, 0)
+        permute_planes(0, 1)
         for m in range(RESIDUALS_BY_TENSOR):
             residual_by_tensor(m, 0)
-        permute_planes(0, 1)
-        transpose_h(0, 1)
-        transpose_h(1, 1)
-        permute_words(0, 1, 1)
-        quantise_h(1)
-        first_matmul(0, by_pass=True)
+        first_matmul(0)
+        permute_planes(1, 0)
         permute_planes(1, 1)
         permute_words(1)
 

@@ -26,6 +26,7 @@ F_CHUNKS = F // K_PASS
 D_HALVES = D // N_TILE
 PLANES_PER_TILE = 4
 RESIDUALS_BY_TENSOR = 2
+LAG = 4
 PACK = 4
 HALF = TOKENS // 2
 
@@ -48,10 +49,15 @@ def tile_ffnn_encoder_pc_kernel(
         psum_o = ctx.enter_context(tc.psum_pool(name="psum_o", bufs=2))
 
         x_pairs = [keep.tile([P, 2, D], BF16, name="x_pair%d" % i) for i in range(2)]
-        w1_raw = [
-            keep.tile([P, D_PASSES, N_TILE], U32, name="w1_raw%d" % g, align_bytes=64)
-            for g in range(F_CHUNKS)
-        ]
+        w1_groups = [(0,), (1,), (2, 3), (4, 5), (6, 7)]
+        w1_raw = {}
+        for group in w1_groups:
+            tile = keep.tile(
+                [P, D_PASSES, len(group) * N_TILE], U32, name="w1_raw%d" % group[0], align_bytes=64
+            )
+            for i, g in enumerate(group):
+                w1_raw[g] = tile[:, :, i * N_TILE : (i + 1) * N_TILE]
+            w1_raw[group] = tile
         w1_words = [
             keep.tile([P, D_PASSES, N_TILE], U32, name="w1_words%d" % g, align_bytes=64)
             for g in range(F_CHUNKS)
@@ -114,11 +120,11 @@ def tile_ffnn_encoder_pc_kernel(
                 in_=h_rows[HALF * i : HALF * (i + 1), :].rearrange("(e p) k -> p e k", e=2),
             )
 
-        def load_w1_chunk(g):
+        def load_w1(group):
             by_partition = W1_words.rearrange("c p n t -> p c (n t)")
+            first, past = 4 * N_TILE * group[0], 4 * N_TILE * (group[-1] + 1)
             nc.sync.dma_start(
-                out=w1_raw[g][:].bitcast(I32),
-                in_=by_partition[:, :, 4 * N_TILE * g : 4 * N_TILE * (g + 1)].bitcast(I32),
+                out=w1_raw[group][:].bitcast(I32), in_=by_partition[:, :, first:past].bitcast(I32)
             )
 
         def load_w2_chunk(g):
@@ -145,7 +151,7 @@ def tile_ffnn_encoder_pc_kernel(
 
         load_h(0)
         load_h(1)
-        load_w1_chunk(0)
+        load_w1(w1_groups[0])
         nc.sync.dma_start(
             out=bias_rows[0:F_CHUNKS, :], in_=b1.rearrange("(r c) -> r c", c=N_TILE)
         )
@@ -155,14 +161,14 @@ def tile_ffnn_encoder_pc_kernel(
         )
         for c in range(D_PASSES):
             load_w1_planes(c)
-        for g in range(1, 4):
-            load_w1_chunk(g)
+        for group in w1_groups[1:4]:
+            load_w1(group)
         for j in range(F_CHUNKS // PLANES_PER_TILE):
             load_w2_planes(j)
         for g in range(F_CHUNKS):
             load_w2_chunk(g)
-            if g + 4 < F_CHUNKS:
-                load_w1_chunk(g + 4)
+            if g == 0:
+                load_w1(w1_groups[4])
         nc.sync.dma_start(out=g2_bc[:], in_=g2.partition_broadcast(P))
         nc.sync.dma_start(out=beta2_bc[:], in_=beta2.partition_broadcast(P))
 
@@ -216,7 +222,7 @@ def tile_ffnn_encoder_pc_kernel(
             tokens = slice((m % 2) * P, (m % 2 + 1) * P)
             words = h_grouped[m // 2][:].rearrange("p c n k -> p (c n k)").bitcast(F32)
             words = words.rearrange("p (c n u) -> p c n u", c=D_PASSES, u=2)
-            copy = nc.vector.tensor_copy if m % 2 == 0 else nc.scalar.copy
+            copy = nc.vector.tensor_copy if m == 0 else nc.scalar.copy
             copy(out=words[:, :, tokens, :], in_=bank[:].rearrange("p c u n -> p c n u"))
 
         def quantise_h(i):
@@ -384,8 +390,8 @@ def tile_ffnn_encoder_pc_kernel(
                     op1=MULT,
                 )
 
-            def finish(half):
-                cols = slice(half * N_TILE, (half + 1) * N_TILE)
+            def finish(i):
+                cols = pieces[m][i]
                 nc.vector.scalar_tensor_tensor(
                     out=result[:, cols],
                     in0=scaled[:, cols],
@@ -398,14 +404,16 @@ def tile_ffnn_encoder_pc_kernel(
 
             return add_residual, add_two_sums, statistics, scale, finish
 
-        for m in range(TOK_TILES):
-            transpose_h(m)
-            if m % 2 == 1:
-                quantise_h(m // 2)
+        transpose_h(0)
+        transpose_h(1)
+        quantise_h(0)
+        permute_words(0)
+        transpose_h(2)
+        transpose_h(3)
+        quantise_h(1)
         b1_to_partitions()
         broadcast_b2(0)
         broadcast_b2(1)
-        permute_words(0)
         permute_planes(0, 0)
         permute_planes(0, 1)
         for m in range(RESIDUALS_BY_TENSOR):
@@ -432,16 +440,16 @@ def tile_ffnn_encoder_pc_kernel(
                 interleave(g - 1, 1)
             if 0 < g < last - 1:
                 permute_words(g + 2)
-            if g < len(by_vector):
-                residual_by_vector(*by_vector[g])
+            if 0 <= g - 2 < len(by_vector):
+                residual_by_vector(*by_vector[g - 2])
             if g >= 1:
                 quantise_hid(g - 1, 0)
                 quantise_hid(g - 1, 1)
-            if g >= 2:
-                second_matmul(0, accs[0], [g - 2])
+            if g >= LAG:
+                second_matmul(0, accs[0], [g - LAG])
 
         accs[1] = open_out_banks(psum_a, 1)
-        second_matmul(0, accs[0], [last - 1])
+        second_matmul(0, accs[0], range(F_CHUNKS - LAG, last))
         second_matmul(1, accs[1], range(1))
         interleave(last, 0)
         quantise_hid(last, 0)
@@ -467,6 +475,6 @@ def tile_ffnn_encoder_pc_kernel(
             statistics()
             scale()
             if m in (0, TOK_TILES - 1):
-                finish(0)
-                finish(1)
+                for i in range(len(pieces[m])):
+                    finish(i)
             finish_before = finish

@@ -49,15 +49,10 @@ def tile_ffnn_encoder_pc_kernel(
         psum_o = ctx.enter_context(tc.psum_pool(name="psum_o", bufs=2))
 
         x_pairs = [keep.tile([P, 2, D], BF16, name="x_pair%d" % i) for i in range(2)]
-        w1_groups = [(0,), (1,), (2, 3), (4, 5), (6, 7)]
-        w1_raw = {}
-        for group in w1_groups:
-            tile = keep.tile(
-                [P, D_PASSES, len(group) * N_TILE], U32, name="w1_raw%d" % group[0], align_bytes=64
-            )
-            for i, g in enumerate(group):
-                w1_raw[g] = tile[:, :, i * N_TILE : (i + 1) * N_TILE]
-            w1_raw[group] = tile
+        w1_raw = [
+            keep.tile([P, D_PASSES, N_TILE], U32, name="w1_raw%d" % g, align_bytes=64)
+            for g in range(F_CHUNKS)
+        ]
         w1_words = [
             keep.tile([P, D_PASSES, N_TILE], U32, name="w1_words%d" % g, align_bytes=64)
             for g in range(F_CHUNKS)
@@ -120,11 +115,11 @@ def tile_ffnn_encoder_pc_kernel(
                 in_=h_rows[HALF * i : HALF * (i + 1), :].rearrange("(e p) k -> p e k", e=2),
             )
 
-        def load_w1(group):
+        def load_w1_chunk(g):
             by_partition = W1_words.rearrange("c p n t -> p c (n t)")
-            first, past = 4 * N_TILE * group[0], 4 * N_TILE * (group[-1] + 1)
             nc.sync.dma_start(
-                out=w1_raw[group][:].bitcast(I32), in_=by_partition[:, :, first:past].bitcast(I32)
+                out=w1_raw[g][:].bitcast(I32),
+                in_=by_partition[:, :, 4 * N_TILE * g : 4 * N_TILE * (g + 1)].bitcast(I32),
             )
 
         def load_w2_chunk(g):
@@ -151,7 +146,7 @@ def tile_ffnn_encoder_pc_kernel(
 
         load_h(0)
         load_h(1)
-        load_w1(w1_groups[0])
+        load_w1_chunk(0)
         nc.sync.dma_start(
             out=bias_rows[0:F_CHUNKS, :], in_=b1.rearrange("(r c) -> r c", c=N_TILE)
         )
@@ -161,14 +156,14 @@ def tile_ffnn_encoder_pc_kernel(
         )
         for c in range(D_PASSES):
             load_w1_planes(c)
-        for group in w1_groups[1:4]:
-            load_w1(group)
+        for g in range(1, 6):
+            load_w1_chunk(g)
         for j in range(F_CHUNKS // PLANES_PER_TILE):
             load_w2_planes(j)
         for g in range(F_CHUNKS):
             load_w2_chunk(g)
-            if g == 0:
-                load_w1(w1_groups[4])
+            if g + 6 < F_CHUNKS:
+                load_w1_chunk(g + 6)
         nc.sync.dma_start(out=g2_bc[:], in_=g2.partition_broadcast(P))
         nc.sync.dma_start(out=beta2_bc[:], in_=beta2.partition_broadcast(P))
 
@@ -254,31 +249,36 @@ def tile_ffnn_encoder_pc_kernel(
         hid_tiles = {}
         grouped_tiles = {}
 
-        def first_matmul(g, first=0, width=TOKENS):
+        def first_matmul(g, first=0, width=TOKENS, by_pass=False):
             if first == 0:
                 hid_tiles[g] = stream.tile([P, PACK, TOKENS], BF16, name="hid")
             tokens = slice(first, first + width)
             x, q = divmod(g, 2)
-            for t in range(PACK):
-                acc = psum_a.tile([P, width], F32, tag="bank", name="hid_acc")
-                for c in range(D_PASSES):
-                    nc.tensor.matmul_mx(
-                        out=acc[:],
-                        lhsT=w1_words[g][:, c, t * P : (t + 1) * P].bitcast(FP8X4),
-                        lhsT_scale=w1_planes[q][
-                            4 * x : P, c * K_PASS + t * P : c * K_PASS + (t + 1) * P
-                        ],
-                        rhs=hq_words[c][:, tokens].bitcast(FP8X4),
-                        rhs_scale=hq_scales[c][:, tokens],
-                        start=(c == 0),
-                        stop=(c == D_PASSES - 1),
-                    )
-                nc.scalar.activation(
-                    out=hid_tiles[g][:, t, tokens],
-                    in_=acc[:],
-                    func=ACT.Relu,
-                    bias=b1_cols[:, t, g : g + 1],
+            order = [(t, c) for t in range(PACK) for c in range(D_PASSES)]
+            if by_pass:
+                order = [(t, c) for c in range(D_PASSES) for t in range(PACK)]
+            banks = {}
+            for t, c in order:
+                if c == 0:
+                    banks[t] = psum_a.tile([P, width], F32, tag="bank", name="hid_acc")
+                nc.tensor.matmul_mx(
+                    out=banks[t][:],
+                    lhsT=w1_words[g][:, c, t * P : (t + 1) * P].bitcast(FP8X4),
+                    lhsT_scale=w1_planes[q][
+                        4 * x : P, c * K_PASS + t * P : c * K_PASS + (t + 1) * P
+                    ],
+                    rhs=hq_words[c][:, tokens].bitcast(FP8X4),
+                    rhs_scale=hq_scales[c][:, tokens],
+                    start=(c == 0),
+                    stop=(c == D_PASSES - 1),
                 )
+                if c == D_PASSES - 1:
+                    nc.scalar.activation(
+                        out=hid_tiles[g][:, t, tokens],
+                        in_=banks[t][:],
+                        func=ACT.Relu,
+                        bias=b1_cols[:, t, g : g + 1],
+                    )
 
         def interleave(g, half):
             if half == 0:
@@ -415,11 +415,11 @@ def tile_ffnn_encoder_pc_kernel(
         broadcast_b2(0)
         broadcast_b2(1)
         permute_planes(0, 0)
+        permute_planes(1, 0)
         permute_planes(0, 1)
         for m in range(RESIDUALS_BY_TENSOR):
             residual_by_tensor(m, 0)
-        first_matmul(0)
-        permute_planes(1, 0)
+        first_matmul(0, by_pass=True)
         permute_planes(1, 1)
         permute_words(1)
 
@@ -429,6 +429,8 @@ def tile_ffnn_encoder_pc_kernel(
         accs = {0: open_out_banks(psum_o, 0)}
         for g in range(F_CHUNKS):
             if g == 0:
+                for i in range(3):
+                    residual_by_vector(*by_vector[i])
                 permute_words(2)
             elif g < last:
                 first_matmul(g)
@@ -440,8 +442,8 @@ def tile_ffnn_encoder_pc_kernel(
                 interleave(g - 1, 1)
             if 0 < g < last - 1:
                 permute_words(g + 2)
-            if 0 <= g - 2 < len(by_vector):
-                residual_by_vector(*by_vector[g - 2])
+            if 3 <= g - 5 + 3 < len(by_vector):
+                residual_by_vector(*by_vector[g - 5 + 3])
             if g >= 1:
                 quantise_hid(g - 1, 0)
                 quantise_hid(g - 1, 1)

from contextlib import ExitStack

import concourse.mybir as mybir
from concourse.masks import make_identity

F32 = mybir.dt.float32
BF16 = mybir.dt.bfloat16
I32 = mybir.dt.int32
U32 = mybir.dt.uint32
U8 = mybir.dt.uint8
FP8X4 = mybir.dt.float8_e4m3fn_x4
ADD = mybir.AluOpType.add
MULT = mybir.AluOpType.mult
ACT = mybir.ActivationFunctionType

P = 128
K_PASS = 512
N_TILE = 512
TOKENS = 512
D = 1024
F = 4096
EPS = 1e-3
TOK_TILES = TOKENS // P
D_PASSES = D // K_PASS
F_CHUNKS = F // K_PASS
D_HALVES = D // N_TILE
PLANES_PER_TILE = 4
RESIDUALS_BY_TENSOR = 2
LAG = 4
PACK = 4
HALF = TOKENS // 2

FLOPS = 2 * TOKENS * D * F * 2


def tile_ffnn_encoder_pc_kernel(
    tc, h_attn, W1_words, W1_scales, b1, W2_words, W2_scales, b2, g2, beta2, out
):
    nc = tc.nc
    h_rows = h_attn.flatten_outer_dims()
    out_rows = out.flatten_outer_dims()

    with ExitStack() as ctx:
        ctx.enter_context(tc.manual_schedule())
        keep = ctx.enter_context(tc.tile_pool(name="keep", bufs=1))
        stream = ctx.enter_context(tc.tile_pool(name="stream", bufs=3))
        norm = ctx.enter_context(tc.tile_pool(name="norm", bufs=2))
        psum_a = ctx.enter_context(tc.psum_pool(name="psum_a", bufs=6))
        psum_o = ctx.enter_context(tc.psum_pool(name="psum_o", bufs=2))

        x_pairs = [keep.tile([P, 2, D], BF16, name="x_pair%d" % i) for i in range(2)]
        w1_raw = [
            keep.tile([P, D_PASSES, N_TILE], U32, name="w1_raw%d" % g, align_bytes=64)
            for g in range(F_CHUNKS)
        ]
        w1_words = [
            keep.tile([P, D_PASSES, N_TILE], U32, name="w1_words%d" % g, align_bytes=64)
            for g in range(F_CHUNKS)
        ]
        w2_words = [
            keep.tile([P, D], U32, name="w2_words%d" % g, align_bytes=64) for g in range(F_CHUNKS)
        ]
        w1_raw_planes = keep.tile([P, D_PASSES, 2 * K_PASS], U8, name="w1_raw_planes", align_bytes=64)
        w1_planes = [
            keep.tile([P, D_PASSES * K_PASS], U8, name="w1_planes%d" % q, align_bytes=64)
            for q in range(2)
        ]
        w2_planes = [
            keep.tile([P, D], U8, name="w2_planes%d" % j, align_bytes=64)
            for j in range(F_CHUNKS // PLANES_PER_TILE)
        ]
        h_grouped = [
            keep.tile([P, D_PASSES, HALF, PACK], BF16, name="h_grouped%d" % i, align_bytes=64)
            for i in range(2)
        ]
        hq_words = [
            keep.tile([P, TOKENS], U32, name="hq_words%d" % c, align_bytes=64)
            for c in range(D_PASSES)
        ]
        hq_scales = [
            keep.tile([P, TOKENS], U8, name="hq_scales%d" % c, align_bytes=64)
            for c in range(D_PASSES)
        ]
        hidq_words = [
            keep.tile([P, TOKENS], U32, name="hidq_words%d" % g, align_bytes=64)
            for g in range(F_CHUNKS)
        ]
        hidq_scales = [
            keep.tile([P, TOKENS], U8, name="hidq_scales%d" % g, align_bytes=64)
            for g in range(F_CHUNKS)
        ]
        bias_rows = keep.tile([P, N_TILE], BF16, name="bias_rows")
        b1_cols = keep.tile([P, PACK, F_CHUNKS], F32, name="b1_cols")
        res = [keep.tile([P, D], F32, name="res%d" % m) for m in range(TOK_TILES)]
        b2_bc = keep.tile([P, D], BF16, name="b2_bc")
        g2_bc = keep.tile([P, D], BF16, name="g2_bc")
        beta2_bc = keep.tile([P, D], BF16, name="beta2_bc")
        ident_f32 = keep.tile([P, P], F32, name="ident_f32")
        ident_bf16 = keep.tile([P, P], BF16, name="ident_bf16")
        eps = keep.tile([P, 1], F32, name="eps")
        first_rsqrt = keep.tile([P, 1], F32, name="first_rsqrt")

        nc.vector.memset(bias_rows[:], 0.0)
        nc.vector.memset(eps[:], EPS)
        nc.vector.memset(w1_raw_planes[:].rearrange("p c n -> p (c n)").bitcast(I32), 0)
        for plane_tile in w2_planes:
            nc.vector.memset(plane_tile[:].bitcast(I32), 0)
        make_identity(nc, ident_bf16[:])
        make_identity(nc, ident_f32[:])
        nc.scalar.activation(out=first_rsqrt[:], in_=eps[:], func=ACT.Abs_reciprocal_sqrt)

        def load_h(i):
            nc.sync.dma_start(
                out=x_pairs[i][:],
                in_=h_rows[HALF * i : HALF * (i + 1), :].rearrange("(e p) k -> p e k", e=2),
            )

        def load_w1_chunk(g):
            by_partition = W1_words.rearrange("c p n t -> p c (n t)")
            nc.sync.dma_start(
                out=w1_raw[g][:].bitcast(I32),
                in_=by_partition[:, :, 4 * N_TILE * g : 4 * N_TILE * (g + 1)].bitcast(I32),
            )

        def load_w2_chunk(g):
            nc.sync.dma_start(
                out=w2_words[g][:].bitcast(I32),
                in_=W2_words[g].rearrange("p n t -> p (n t)").bitcast(I32),
            )

        def load_w1_planes(c):
            for quadrant in range(4):
                rows = W1_scales[c, 4 * quadrant : 4 * quadrant + 4, :]
                nc.sync.dma_start(
                    out=w1_raw_planes[32 * quadrant : 32 * quadrant + 16, c, :].bitcast(I32),
                    in_=rows.rearrange("r (x n) -> x r n", n=2 * K_PASS).bitcast(I32),
                )

        def load_w2_planes(j):
            scales = W2_scales[PLANES_PER_TILE * j : PLANES_PER_TILE * (j + 1)]
            for quadrant in range(4):
                nc.sync.dma_start(
                    out=w2_planes[j][32 * quadrant : 32 * quadrant + 16, :].bitcast(I32),
                    in_=scales[:, 4 * quadrant : 4 * quadrant + 4, :].bitcast(I32),
                )

        load_h(0)
        load_h(1)
        load_w1_chunk(0)
        nc.sync.dma_start(
            out=bias_rows[0:F_CHUNKS, :], in_=b1.rearrange("(r c) -> r c", c=N_TILE)
        )
        nc.sync.dma_start(
            out=bias_rows[F_CHUNKS : F_CHUNKS + D_HALVES, :],
            in_=b2.rearrange("(r c) -> r c", c=N_TILE),
        )
        for c in range(D_PASSES):
            load_w1_planes(c)
        for g in range(1, 6):
            load_w1_chunk(g)
        for j in range(F_CHUNKS // PLANES_PER_TILE):
            load_w2_planes(j)
        for g in range(F_CHUNKS):
            load_w2_chunk(g)
            if g + 6 < F_CHUNKS:
                load_w1_chunk(g + 6)
        nc.sync.dma_start(out=g2_bc[:], in_=g2.partition_broadcast(P))
        nc.sync.dma_start(out=beta2_bc[:], in_=beta2.partition_broadcast(P))

        def b1_to_partitions():
            bank = psum_a.tile([P, 2 * PACK, P], BF16, tag="bank", name="b1_bank")
            by_slot = bias_rows[:].rearrange("r (p t) -> r t p", t=PACK)
            for t in range(PACK):
                nc.tensor.transpose(bank[:, t, :], by_slot[:, t, :], ident_bf16[:])
            nc.scalar.copy(out=b1_cols[:], in_=bank[:, 0:PACK, 0:F_CHUNKS])

        def spread_b2(bank, half, start, stop):
            row = F_CHUNKS + half
            nc.tensor.matmul(
                out=bank[:],
                lhsT=ident_bf16[:, row : row + 1].to_broadcast([P, P]),
                rhs=bias_rows[:],
                start=start,
                stop=stop,
            )

        def broadcast_b2(half):
            bank = psum_a.tile([P, N_TILE], F32, tag="bank", name="b2_bank")
            spread_b2(bank, half, True, True)
            nc.scalar.copy(out=b2_bc[:, half * N_TILE : (half + 1) * N_TILE], in_=bank[:])

        def residual_by_tensor(m, half):
            cols = slice(half * N_TILE, (half + 1) * N_TILE)
            bank = psum_o.tile([P, N_TILE], F32, tag="bank", name="res_bank")
            nc.tensor.matmul(
                out=bank[:], lhsT=ident_bf16[:], rhs=x_pairs[m // 2][:, m % 2, cols], start=True, stop=False
            )
            spread_b2(bank, half, False, True)
            nc.scalar.copy(out=res[m][:, cols], in_=bank[:])

        def residual_by_vector(m, half):
            cols = slice(half * N_TILE, (half + 1) * N_TILE)
            nc.vector.tensor_tensor(
                out=res[m][:, cols], in0=x_pairs[m // 2][:, m % 2, cols], in1=b2_bc[:, cols], op=ADD
            )

        def transpose_h(m):
            x_as_words = x_pairs[m // 2][:, m % 2, :].bitcast(F32)
            bank = psum_a.tile([P, D_PASSES, 2, P], F32, tag="bank", name="hT_bank")
            for c in range(D_PASSES):
                for u in range(2):
                    nc.tensor.transpose(
                        bank[:, c, u, :],
                        x_as_words[:, 256 * c + u : 256 * (c + 1) : 2],
                        ident_f32[:],
                    )
            tokens = slice((m % 2) * P, (m % 2 + 1) * P)
            words = h_grouped[m // 2][:].rearrange("p c n k -> p (c n k)").bitcast(F32)
            words = words.rearrange("p (c n u) -> p c n u", c=D_PASSES, u=2)
            copy = nc.vector.tensor_copy if m == 0 else nc.scalar.copy
            copy(out=words[:, :, tokens, :], in_=bank[:].rearrange("p c u n -> p c n u"))

        def quantise_h(i):
            cols = slice(HALF * i, HALF * (i + 1))
            for c in range(D_PASSES):
                nc.vector.quantize_mx(
                    out=hq_words[c][:, cols].bitcast(FP8X4),
                    scales=hq_scales[c][:, cols],
                    in_=h_grouped[i][:, c, :, :].rearrange("p n k -> p (n k)"),
                )

        def permute_planes(q, c):
            nc.vector.tensor_copy(
                out=w1_planes[q][:, c * K_PASS : (c + 1) * K_PASS].rearrange(
                    "p (t m) -> p m t", t=PACK
                ),
                in_=w1_raw_planes[:, c, K_PASS * q : K_PASS * (q + 1)].rearrange(
                    "p (m t) -> p m t", t=PACK
                ),
            )

        def permute_words(g, first=0, passes=D_PASSES):
            c = slice(first, first + passes)
            nc.vector.tensor_copy(
                out=w1_words[g][:, c, :].bitcast(I32).rearrange("p c (t m) -> p c m t", t=PACK),
                in_=w1_raw[g][:, c, :].bitcast(I32).rearrange("p c (m t) -> p c m t", t=PACK),
            )

        hid_tiles = {}
        grouped_tiles = {}

        def first_matmul(g, first=0, width=TOKENS, by_pass=False):
            if first == 0:
                hid_tiles[g] = stream.tile([P, PACK, TOKENS], BF16, name="hid")
            tokens = slice(first, first + width)
            x, q = divmod(g, 2)
            order = [(t, c) for t in range(PACK) for c in range(D_PASSES)]
            if by_pass:
                order = [(t, c) for c in range(D_PASSES) for t in range(PACK)]
            banks = {}
            for t, c in order:
                if c == 0:
                    banks[t] = psum_a.tile([P, width], F32, tag="bank", name="hid_acc")
                nc.tensor.matmul_mx(
                    out=banks[t][:],
                    lhsT=w1_words[g][:, c, t * P : (t + 1) * P].bitcast(FP8X4),
                    lhsT_scale=w1_planes[q][
                        4 * x : P, c * K_PASS + t * P : c * K_PASS + (t + 1) * P
                    ],
                    rhs=hq_words[c][:, tokens].bitcast(FP8X4),
                    rhs_scale=hq_scales[c][:, tokens],
                    start=(c == 0),
                    stop=(c == D_PASSES - 1),
                )
                if c == D_PASSES - 1:
                    nc.scalar.activation(
                        out=hid_tiles[g][:, t, tokens],
                        in_=banks[t][:],
                        func=ACT.Relu,
                        bias=b1_cols[:, t, g : g + 1],
                    )

        def interleave(g, half):
            if half == 0:
                grouped_tiles[g] = stream.tile(
                    [P, TOKENS, PACK], BF16, name="hid_grouped", align_bytes=64
                )
            cols = slice(HALF * half, HALF * (half + 1))
            nc.vector.tensor_copy(
                out=grouped_tiles[g][:, cols, :].rearrange("p (n i) t -> p n t i", i=4),
                in_=hid_tiles[g][:, :, cols].rearrange("p t (n i) -> p n t i", i=4),
            )

        def quantise_hid(g, half):
            cols = slice(HALF * half, HALF * (half + 1))
            nc.vector.quantize_mx(
                out=hidq_words[g][:, cols].bitcast(FP8X4),
                scales=hidq_scales[g][:, cols],
                in_=grouped_tiles[g][:, cols, :].rearrange("p n t -> p (n t)"),
            )

        half_row = slice(0, N_TILE), slice(N_TILE, D)
        pieces = [half_row] * (TOK_TILES - 1)
        pieces.append((slice(0, N_TILE), slice(N_TILE, 3 * N_TILE // 2), slice(3 * N_TILE // 2, D)))

        def open_out_banks(pool, m):
            return [
                pool.tile([P, cols.stop - cols.start], F32, tag="bank", name="out_acc")
                for cols in pieces[m]
            ]

        def second_matmul(m, accs, chunks, which=(0, 1)):
            rows = slice(m * P, (m + 1) * P)
            for g in chunks:
                for i in which:
                    offset = 4 * (g % PLANES_PER_TILE)
                    cols = pieces[m][i]
                    nc.tensor.matmul_mx(
                        out=accs[i][:],
                        lhsT=hidq_words[g][:, rows].bitcast(FP8X4),
                        lhsT_scale=hidq_scales[g][:, rows],
                        rhs=w2_words[g][:, cols].bitcast(FP8X4),
                        rhs_scale=w2_planes[g // PLANES_PER_TILE][offset:P, cols],
                        start=(g == 0),
                        stop=(g == F_CHUNKS - 1),
                    )

        def layer_norm(m, accs):
            r = norm.tile([P, D], F32, name="r")
            r_sums = norm.tile([P, 3], F32, name="r_sums")
            two_sums = norm.tile([P, 1], F32, name="two_sums")
            neg_mean = norm.tile([P, 1], F32, name="neg_mean")
            squares = norm.tile([P, D], BF16, name="squares")
            sum_sq = norm.tile([P, 1], F32, name="sum_sq")
            scaled = norm.tile([P, D], F32, name="scaled")
            rstd = norm.tile([P, 1], F32, name="rstd")
            result = norm.tile([P, D], F32, name="result")

            def add_residual(i):
                cols = pieces[m][i]
                nc.vector.scalar_tensor_tensor(
                    out=r[:, cols],
                    in0=accs[i][:],
                    scalar=1.0,
                    in1=res[m][:, cols],
                    op0=MULT,
                    op1=ADD,
                    accum_out=r_sums[:, i : i + 1],
                )

            def add_two_sums():
                nc.vector.tensor_scalar(
                    out=two_sums[:], in0=r_sums[:, 0:1], scalar1=r_sums[:, 1:2], scalar2=None, op0=ADD
                )

            def statistics():
                first, second = r_sums[:, 0:1], r_sums[:, 1:2]
                if len(pieces[m]) == 3:
                    first, second = two_sums[:], r_sums[:, 2:3]
                nc.vector.tensor_scalar(
                    out=neg_mean[:],
                    in0=first,
                    scalar1=second,
                    scalar2=-1.0 / D,
                    op0=ADD,
                    op1=MULT,
                )
                nc.scalar.activation(
                    out=squares[:],
                    in_=r[:],
                    func=ACT.Square,
                    bias=neg_mean[:, 0:1],
                    accum_out=sum_sq[:],
                )
                nc.scalar.activation(
                    out=rstd[:],
                    in_=sum_sq[:],
                    func=ACT.Abs_reciprocal_sqrt,
                    bias=eps[:, 0:1],
                    scale=1.0 / D,
                )

            def scale():
                nc.vector.scalar_tensor_tensor(
                    out=scaled[:],
                    in0=r[:],
                    scalar=neg_mean[:, 0:1],
                    in1=g2_bc[:],
                    op0=ADD,
                    op1=MULT,
                )

            def finish(i):
                cols = pieces[m][i]
                nc.vector.scalar_tensor_tensor(
                    out=result[:, cols],
                    in0=scaled[:, cols],
                    scalar=rstd[:, 0:1],
                    in1=beta2_bc[:, cols],
                    op0=MULT,
                    op1=ADD,
                )
                nc.sync.dma_start(out=out_rows[m * P : (m + 1) * P, cols], in_=result[:, cols])

            return add_residual, add_two_sums, statistics, scale, finish

        transpose_h(0)
        transpose_h(1)
        quantise_h(0)
        permute_words(0)
        transpose_h(2)
        transpose_h(3)
        quantise_h(1)
        b1_to_partitions()
        broadcast_b2(0)
        broadcast_b2(1)
        permute_planes(0, 0)
        permute_planes(1, 0)
        permute_planes(0, 1)
        for m in range(RESIDUALS_BY_TENSOR):
            residual_by_tensor(m, 0)
        first_matmul(0, by_pass=True)
        permute_planes(1, 1)
        permute_words(1)

        last = F_CHUNKS - 1
        by_vector = [(m, 1) for m in range(RESIDUALS_BY_TENSOR)]
        by_vector += [(m, half) for m in range(RESIDUALS_BY_TENSOR, TOK_TILES) for half in range(2)]
        accs = {0: open_out_banks(psum_o, 0)}
        for g in range(F_CHUNKS):
            if g == 0:
                for i in range(3):
                    residual_by_vector(*by_vector[i])
                permute_words(2)
            elif g < last:
                first_matmul(g)
            else:
                first_matmul(g, 0, HALF)
                first_matmul(g, HALF, HALF)
            if g >= 1:
                interleave(g - 1, 0)
                interleave(g - 1, 1)
            if 0 < g < last - 1:
                permute_words(g + 2)
            if 3 <= g - 5 + 3 < len(by_vector):
                residual_by_vector(*by_vector[g - 5 + 3])
            if g >= 1:
                quantise_hid(g - 1, 0)
                quantise_hid(g - 1, 1)
            if g >= LAG:
                second_matmul(0, accs[0], [g - LAG])

        accs[1] = open_out_banks(psum_a, 1)
        second_matmul(0, accs[0], range(F_CHUNKS - LAG, last))
        second_matmul(1, accs[1], range(1))
        interleave(last, 0)
        quantise_hid(last, 0)
        interleave(last, 1)
        quantise_hid(last, 1)
        second_matmul(0, accs[0], [last])
        second_matmul(1, accs[1], range(1, F_CHUNKS))

        for m in range(TOK_TILES):
            if 2 <= m + 1 < TOK_TILES:
                accs[m + 1] = open_out_banks(psum_a, m + 1)
                for i in range(len(pieces[m + 1])):
                    second_matmul(m + 1, accs[m + 1], range(F_CHUNKS), [i])
            add_residual, add_two_sums, statistics, scale, finish = layer_norm(m, accs[m])
            add_residual(0)
            if m >= 2:
                finish_before(0)
                finish_before(1)
            add_residual(1)
            if len(pieces[m]) == 3:
                add_two_sums()
                add_residual(2)
            statistics()
            scale()
            if m in (0, TOK_TILES - 1):
                for i in range(len(pieces[m])):
                    finish(i)
            finish_before = finish
